import numpy as np
import ml_dtypes


def mxq(x, axis, fmt="e4m3"):
    dtype, down = {"e4m3": (ml_dtypes.float8_e4m3fn, 7), "e5m2": (ml_dtypes.float8_e5m2, 14)}[fmt]
    v = np.moveaxis(np.asarray(x, np.float32).astype(ml_dtypes.bfloat16).astype(np.float64), axis, -1)
    blocks = v.reshape(v.shape[:-1] + (-1, 32))
    amax = np.abs(blocks).max(-1, keepdims=True)
    byte = np.maximum(np.where(amax > 0, np.frexp(amax)[1] - 1 + 127, 0) - down, 1)
    scale = np.exp2(byte - 127.0)
    codes = (blocks / scale).astype(np.float32).astype(dtype).astype(np.float64)
    return np.moveaxis((codes * scale).reshape(v.shape), -1, axis)


WIDE = False


def mx_kscale(k):
    if not WIDE:
        return np.ones(k)
    levels = np.array([10, -10, 5, -5, 0])
    a = np.random.permutation(np.resize(levels, k // 512 * 4)).reshape(k // 512, 4)
    idx = np.arange(k)
    return np.exp2(a[idx // 512, idx % 128 // 32])


BF16 = ml_dtypes.bfloat16


def bf(x):
    return np.asarray(x, np.float32).astype(BF16)


def f64(x):
    return np.asarray(x).astype(np.float64)


E2M1 = np.array([0.0, 0.5, 1.0, 1.5, 2.0, 3.0, 4.0, 6.0, -0.0, -0.5, -1.0, -1.5, -2.0, -3.0, -4.0, -6.0])


def pack_weight(w, fmt):
    k, n = w.shape
    w = f64(bf(w)).reshape(k // 32, 32, n)
    amax = np.abs(w).max(1)
    if fmt == "e4m3":
        byte = np.frexp(amax)[1] - 1 + 127 - 7
    else:
        mant, ex = np.frexp(amax / 6.0)
        byte = np.where(mant > 0.5, ex, ex - 1) + 127
    byte = np.clip(np.where(amax > 0, byte, 1), 1, 254)
    scaled = (w * np.exp2(127.0 - byte)[:, None, :]).reshape(k, n).astype(np.float32)
    by_word = np.ascontiguousarray(scaled.reshape(k // 512, 128, 4, n).transpose(0, 1, 3, 2))
    if fmt == "e4m3":
        words = by_word.astype(ml_dtypes.float8_e4m3fn).view(np.uint8)
    else:
        c = by_word.astype(ml_dtypes.float4_e2m1fn).view(np.uint8) & 0xF
        words = c[..., 0::2] | (c[..., 1::2] << 4)
    return np.ascontiguousarray(words), np.ascontiguousarray(byte.astype(np.uint8).reshape(k // 512, 16, n))


def unpack_weight(words, scales, fmt):
    g, p, n, _ = words.shape
    if fmt == "e4m3":
        vals = np.ascontiguousarray(words).view(ml_dtypes.float8_e4m3fn).astype(np.float64)
    else:
        nib = np.empty((g, p, n, 4), np.uint8)
        nib[..., 0::2] = words & 0xF
        nib[..., 1::2] = words >> 4
        vals = E2M1[nib]
    vals = vals * np.repeat(np.exp2(scales.astype(np.float64) - 127.0), 8, axis=1)[..., None]
    return vals.transpose(0, 1, 3, 2).reshape(g * 512, n)


B, N, D, E, S, H = 2, 512, 512, 4, 128, 2048


def gelu_tanh(v):
    return 0.5 * v * (1.0 + np.tanh(np.sqrt(2.0 / np.pi) * (v + 0.044715 * v**3)))


def setup_inputs():
    t = mx_kscale(H)
    h = bf(gelu_tanh(np.random.standard_normal((B, E, S, H)) * 0.9) * t)
    w2 = np.random.standard_normal((E, H, D)) * 3.0 / np.sqrt(H) / t[:, None]
    w2_words, w2_scales = pack_weight(w2.reshape(-1, D), "e4m3")
    return {"h": h,
            "w2_words": w2_words,
            "w2_scales": w2_scales,
            "b2": bf(np.random.standard_normal((E, D)) * 0.3),
            "x": bf(np.random.standard_normal((B, N, D))),
            "phi": bf(np.random.standard_normal((E, S, D)) * 2.0 / np.sqrt(D))}


def reference(h, w2_words, w2_scales, b2, x, phi):
    w2 = unpack_weight(w2_words, w2_scales, "e4m3").reshape(E, H, D)
    y = (mxq(f64(h), 3, "e4m3") @ w2) + f64(b2)[None, :, None, :]
    logits = f64(x) @ f64(phi).reshape(E * S, D).T
    p = np.exp(logits - logits.max(2, keepdims=True))
    return (mxq(p, 2, "e4m3") @ mxq(y.reshape(B, E * S, D), 1, "e4m3")) / p.sum(2, keepdims=True)

@@ -1,0 +1,264 @@
+from contextlib import ExitStack
+
+import concourse.mybir as mybir
+from concourse.masks import make_identity
+
+F32 = mybir.dt.float32
+BF16 = mybir.dt.bfloat16
+I32 = mybir.dt.int32
+U32 = mybir.dt.uint32
+U8 = mybir.dt.uint8
+FP8X4 = mybir.dt.float8_e4m3fn_x4
+ALU = mybir.AluOpType
+ACT = mybir.ActivationFunctionType
+AXIS = mybir.AxisListType
+
+P = 128
+PACK = 4
+K_PASS = P * PACK
+
+BATCH, EXPERTS, SLOTS, HIDDEN = 2, 4, 128, 2048
+TOKENS, FEAT = 512, 512
+ALL_SLOTS = EXPERTS * SLOTS
+TOKEN_TILES = TOKENS // P
+FEAT_BLOCKS = FEAT // P
+PASSES = HIDDEN // K_PASS
+WORDS = HIDDEN // 2
+PASS_WORDS = K_PASS // 2
+
+COMBINE_LAG = 2
+
+FLOPS = 2 * (BATCH * EXPERTS * SLOTS * HIDDEN * FEAT + 2 * BATCH * TOKENS * ALL_SLOTS * FEAT)
+
+
+def tile_mixtureexpertsmlp_pb_e_kernel(tc, h, w2_words, w2_scales, b2, x, phi, out):
+    nc = tc.nc
+    with ExitStack() as ctx:
+        ctx.enter_context(tc.manual_schedule())
+        keep = ctx.enter_context(tc.tile_pool(name="keep", bufs=1))
+        stage = ctx.enter_context(tc.tile_pool(name="stage", bufs=3))
+        results = ctx.enter_context(tc.tile_pool(name="results", bufs=TOKEN_TILES))
+        psum = ctx.enter_context(tc.psum_pool(name="psum", bufs=4))
+
+        def copy_out(piece, out_ap, in_ap):
+            if piece % 2 == 0:
+                nc.vector.tensor_copy(out=out_ap, in_=in_ap)
+            else:
+                nc.scalar.copy(out=out_ap, in_=in_ap)
+
+        ident_bf = keep.tile([P, P], BF16, name="ident_bf")
+        ident_f32 = keep.tile([P, P], F32, name="ident_f32")
+        make_identity(nc, ident_bf[:])
+        make_identity(nc, ident_f32[:])
+        ones_bf = keep.tile([P, P], BF16, name="ones_bf")
+        nc.vector.memset(ones_bf[:], 1.0)
+        b2_row = keep.tile([P, EXPERTS * FEAT], BF16, name="b2_row")
+        nc.vector.memset(b2_row[:].bitcast(I32), 0)
+        w_scales = keep.tile([P, EXPERTS * PASSES, FEAT], U8, name="w_scales", align_bytes=64)
+        nc.vector.memset(w_scales[:].rearrange("r g n -> r (g n)").bitcast(I32), 0)
+        warm = keep.tile([P, 1], F32, name="warm")
+        nc.vector.memset(warm[:], 0.0)
+        nc.scalar.activation(out=warm[:], in_=warm[:], func=ACT.Exp)
+
+        phi_sb = [keep.tile([P, FEAT], BF16, name="phi_sb%d" % e) for e in range(EXPERTS)]
+        for e in range(EXPERTS):
+            nc.sync.dma_start(out=phi_sb[e][:], in_=phi[e])
+        x_sb = [keep.tile([P, TOKEN_TILES, FEAT], BF16, name="x_sb%d" % b) for b in range(BATCH)]
+        for b in range(BATCH):
+            nc.sync.dma_start(out=x_sb[b][:], in_=x[b].rearrange("(r m) d -> r m d", m=TOKEN_TILES))
+        nc.sync.dma_start(out=b2_row[0:1, :], in_=b2.rearrange("(o e) d -> o (e d)", o=1))
+        h_sb = [[keep.tile([P, HIDDEN], BF16, name="h_sb%d_%d" % (b, e)) for e in range(EXPERTS)] for b in range(BATCH)]
+        for b in range(BATCH):
+            for e in range(EXPERTS):
+                nc.sync.dma_start(out=h_sb[b][e][:], in_=h[b, e])
+        for low_q in range(2):
+            for i in range(4):
+                nc.sync.dma_start(
+                    out=w_scales[32 * low_q + i : P : 64, :, :].bitcast(I32),
+                    in_=w2_scales[:, 4 * low_q + i : 16 : 8, :].rearrange("g q n -> q g n").bitcast(I32),
+                )
+        w_codes = [keep.tile([P, PASSES, FEAT], U32, name="w_codes%d" % e, align_bytes=64) for e in range(EXPERTS)]
+        for e in range(EXPERTS):
+            nc.sync.dma_start(
+                out=w_codes[e][:].bitcast(I32),
+                in_=w2_words[PASSES * e : PASSES * (e + 1)].rearrange("g r n t -> r g (n t)").bitcast(I32),
+            )
+
+        phiT = keep.tile([P, FEAT_BLOCKS, ALL_SLOTS], BF16, name="phiT")
+        xT = [keep.tile([P, TOKEN_TILES, FEAT_BLOCKS, P], BF16, name="xT%d" % b) for b in range(BATCH)]
+        p_bf = [[keep.tile([P, ALL_SLOTS], BF16, name="p_bf%d_%d" % (b, m)) for m in range(TOKEN_TILES)] for b in range(BATCH)]
+        neg_max = keep.tile([P, BATCH * TOKEN_TILES], F32, name="neg_max")
+        p_sum = keep.tile([P, BATCH * TOKEN_TILES], F32, name="p_sum")
+        inv_sum = keep.tile([P, BATCH * TOKEN_TILES], F32, name="inv_sum")
+
+        def transpose_phi(e):
+            flipped = psum.tile([P, FEAT_BLOCKS, P], BF16, tag="small", name="phi_flipped")
+            for c in range(FEAT_BLOCKS):
+                nc.tensor.transpose(flipped[:, c, :], phi_sb[e][:, c * P : (c + 1) * P], ident_bf[:])
+            copy_out(e, phiT[:, :, e * P : (e + 1) * P], flipped[:])
+
+        def transpose_x(b, m):
+            flipped = psum.tile([P, FEAT_BLOCKS, P], BF16, tag="small", name="x_flipped")
+            for c in range(FEAT_BLOCKS):
+                nc.tensor.transpose(flipped[:, c, :], x_sb[b][:, m, c * P : (c + 1) * P], ident_bf[:])
+            copy_out(m, xT[b][:, m, :, :], flipped[:])
+
+        def softmax_numerator(b, m):
+            col = b * TOKEN_TILES + m
+            logits = psum.tile([P, ALL_SLOTS], F32, tag="wide", name="logits")
+            for c in range(FEAT_BLOCKS):
+                nc.tensor.matmul(
+                    out=logits[:], lhsT=xT[b][:, m, c, :], rhs=phiT[:, c, :],
+                    start=(c == 0), stop=(c == FEAT_BLOCKS - 1),
+                )
+            nc.vector.tensor_reduce(
+                out=neg_max[:, col : col + 1], in_=logits[:], axis=AXIS.X, op=ALU.max, negate=True
+            )
+            nc.scalar.activation(
+                out=p_bf[b][m][:], in_=logits[:], func=ACT.Exp,
+                bias=neg_max[:, col : col + 1], scale=1.0, accum_out=p_sum[:, col : col + 1],
+            )
+
+        for e in range(EXPERTS):
+            transpose_phi(e)
+        for b in range(BATCH):
+            for m in range(TOKEN_TILES):
+                transpose_x(b, m)
+            for m in range(TOKEN_TILES):
+                softmax_numerator(b, m)
+
+        bias_sb = keep.tile([P, FEAT_BLOCKS, P, EXPERTS], F32, name="bias_sb")
+        for j in range(FEAT_BLOCKS):
+            spread = psum.tile([P, EXPERTS, P], F32, tag="small", name="bias_spread")
+            for e in range(EXPERTS):
+                first = e * FEAT + j * P
+                nc.tensor.matmul(
+                    out=spread[:, e, :], lhsT=ones_bf[:], rhs=b2_row[:, first : first + P], start=True, stop=True
+                )
+            copy_out(j, bias_sb[:, j, :, :], spread[:].rearrange("s e d -> s d e"))
+
+        p_grouped = [keep.tile([P, TOKEN_TILES, P, PACK], BF16, name="p_grouped%d" % b, align_bytes=64) for b in range(BATCH)]
+        p_codes = [keep.tile([P, TOKEN_TILES, P], U32, name="p_codes%d" % b, align_bytes=64) for b in range(BATCH)]
+        p_scales = [keep.tile([P, TOKEN_TILES, P], U8, name="p_scales%d" % b, align_bytes=64) for b in range(BATCH)]
+
+        def transpose_p(b, m):
+            flipped = psum.tile([P, EXPERTS, P], BF16, tag="small", name="p_flipped")
+            for e in range(EXPERTS):
+                nc.tensor.transpose(flipped[:, e, :], p_bf[b][m][:, e * P : (e + 1) * P], ident_bf[:])
+            copy_out(m, p_grouped[b][:, m, :, :], flipped[:].rearrange("s e r -> s r e"))
+
+        def quantise_p(b, m):
+            nc.vector.quantize_mx(
+                out=p_codes[b][:, m, :].bitcast(FP8X4),
+                scales=p_scales[b][:, m, :],
+                in_=p_grouped[b][:, m, :, :].rearrange("s r e -> s (r e)"),
+            )
+
+        token_tiles = [(b, m) for b in range(BATCH) for m in range(TOKEN_TILES)]
+        for i, (b, m) in enumerate(token_tiles):
+            transpose_p(b, m)
+            if i > 0:
+                quantise_p(*token_tiles[i - 1])
+        quantise_p(*token_tiles[-1])
+        nc.vector.reciprocal(out=inv_sum[:], in_=p_sum[:])
+
+        h_codes = [[keep.tile([P, PASSES, P], U32, name="h_codes%d_%d" % (b, e), align_bytes=64) for e in range(EXPERTS)] for b in range(BATCH)]
+        h_scales = [[keep.tile([P, PASSES, P], U8, name="h_scales%d_%d" % (b, e), align_bytes=64) for e in range(EXPERTS)] for b in range(BATCH)]
+
+        def transpose_h(b, e):
+            words = h_sb[b][e][:].bitcast(F32)
+            grouped = stage.tile([P, PASSES, P, PACK], BF16, name="h_grouped", align_bytes=64)
+            for half in range(2):
+                flipped = psum.tile([P, 2, 2, P], F32, tag="small", name="h_flipped")
+                for gg in range(2):
+                    g = 2 * half + gg
+                    for u in range(2):
+                        nc.tensor.transpose(
+                            flipped[:, gg, u, :],
+                            words[:, PASS_WORDS * g + u : PASS_WORDS * (g + 1) : 2],
+                            ident_f32[:],
+                        )
+                copy_out(
+                    0 if (half == 1 and e % 2 == 1) else 1,
+                    grouped[:, 2 * half : 2 * half + 2, :, :].bitcast(F32),
+                    flipped[:].rearrange("r g u s -> r g s u"),
+                )
+            return grouped
+
+        def quantise_h(b, e, grouped):
+            nc.vector.quantize_mx(
+                out=h_codes[b][e][:].rearrange("r g s -> r (g s)").bitcast(FP8X4),
+                scales=h_scales[b][e][:].rearrange("r g s -> r (g s)"),
+                in_=grouped[:].rearrange("r g s t -> r (g s t)"),
+            )
+
+        waiting = None
+        for b in range(BATCH):
+            for e in range(EXPERTS):
+                grouped = transpose_h(b, e)
+                if waiting is not None:
+                    quantise_h(*waiting)
+                waiting = (b, e, grouped)
+        quantise_h(*waiting)
+
+        y_codes = [keep.tile([P, P], U32, name="y_codes%d" % i, align_bytes=64) for i in range(BATCH * FEAT_BLOCKS)]
+        y_scales = [keep.tile([P, P], U8, name="y_scales%d" % i, align_bytes=64) for i in range(BATCH * FEAT_BLOCKS)]
+        combined = {}
+
+        def first_layer(b, j):
+            cols = slice(j * P, (j + 1) * P)
+            y_psum = psum.tile([P, EXPERTS, P], F32, tag="small", name="y_psum")
+            for e in range(EXPERTS):
+                for g in range(PASSES):
+                    nc.tensor.matmul_mx(
+                        out=y_psum[:, e, :],
+                        lhsT=h_codes[b][e][:, g, :].bitcast(FP8X4),
+                        lhsT_scale=h_scales[b][e][:, g, :],
+                        rhs=w_codes[e][:, g, cols].bitcast(FP8X4),
+                        rhs_scale=w_scales[:, e * PASSES + g, cols],
+                        start=(g == 0),
+                        stop=(g == PASSES - 1),
+                    )
+            y_grouped = stage.tile([P, P, PACK], BF16, name="y_grouped", align_bytes=64)
+            nc.vector.tensor_tensor(
+                out=y_grouped[:], in0=y_psum[:].rearrange("s e d -> s d e"), in1=bias_sb[:, j, :, :], op=ALU.add
+            )
+            nc.vector.quantize_mx(
+                out=y_codes[b * FEAT_BLOCKS + j][:].bitcast(FP8X4),
+                scales=y_scales[b * FEAT_BLOCKS + j][:],
+                in_=y_grouped[:].rearrange("s d e -> s (d e)"),
+            )
+
+        def combine(b, j):
+            for m in range(TOKEN_TILES):
+                if j == 0:
+                    combined[m] = psum.tile([P, FEAT], F32, tag="wide", name="combined")
+                nc.tensor.matmul_mx(
+                    out=combined[m][:, j * P : (j + 1) * P],
+                    lhsT=p_codes[b][:, m, :].bitcast(FP8X4),
+                    lhsT_scale=p_scales[b][:, m, :],
+                    rhs=y_codes[b * FEAT_BLOCKS + j][:].bitcast(FP8X4),
+                    rhs_scale=y_scales[b * FEAT_BLOCKS + j][:],
+                    start=True,
+                    stop=True,
+                )
+
+        def divide_and_store(b, m):
+            col = b * TOKEN_TILES + m
+            result = results.tile([P, FEAT], F32, name="result")
+            if m % 2 == 0:
+                nc.scalar.activation(out=result[:], in_=combined[m][:], func=ACT.Copy, scale=inv_sum[:, col : col + 1])
+            else:
+                nc.vector.tensor_scalar_mul(out=result[:], in0=combined[m][:], scalar1=inv_sum[:, col : col + 1])
+            nc.sync.dma_start(out=out[b].rearrange("(r m) d -> r m d", m=TOKEN_TILES)[:, m, :], in_=result[:])
+
+        blocks = [(b, j) for b in range(BATCH) for j in range(FEAT_BLOCKS)]
+        for i in range(len(blocks) + COMBINE_LAG):
+            if i < len(blocks):
+                first_layer(*blocks[i])
+            if i >= COMBINE_LAG:
+                b, j = blocks[i - COMBINE_LAG]
+                combine(b, j)
+                if j == FEAT_BLOCKS - 1:
+                    for m in range(TOKEN_TILES):
+                        divide_and_store(b, m)

@@ -90,42 +90,130 @@ def tile_mixtureexpertsmlp_pb_e_kernel(tc, h, w2_words, w2_scales, b2, x, phi, o
         neg_max = keep.tile([P, BATCH * TOKEN_TILES], F32, name="neg_max")
         p_sum = keep.tile([P, BATCH * TOKEN_TILES], F32, name="p_sum")
         inv_sum = keep.tile([P, BATCH * TOKEN_TILES], F32, name="inv_sum")
+        p_grouped = [keep.tile([P, TOKEN_TILES, P, PACK], BF16, name="p_grouped%d" % b, align_bytes=64) for b in range(BATCH)]
+        p_codes = [keep.tile([P, TOKEN_TILES, P], U32, name="p_codes%d" % b, align_bytes=64) for b in range(BATCH)]
+        p_scales = [keep.tile([P, TOKEN_TILES, P], U8, name="p_scales%d" % b, align_bytes=64) for b in range(BATCH)]
+        h_grouped = {}
+        h_codes = [[keep.tile([P, PASSES, P], U32, name="h_codes%d_%d" % (b, e), align_bytes=64) for e in range(EXPERTS)] for b in range(BATCH)]
+        h_scales = [[keep.tile([P, PASSES, P], U8, name="h_scales%d_%d" % (b, e), align_bytes=64) for e in range(EXPERTS)] for b in range(BATCH)]
 
-        def transpose_phi(e):
-            flipped = psum.tile([P, FEAT_BLOCKS, P], BF16, tag="small", name="phi_flipped")
+        def new_flipped_bf16():
+            return psum.tile([P, 4, P], BF16, tag="small", name="flipped_bf16")
+
+        def transpose_phi(e, c, flipped):
+            nc.tensor.transpose(flipped[:, c, :], phi_sb[e][:, c * P : (c + 1) * P], ident_bf[:])
+
+        def transpose_x(b, m, c, flipped):
+            nc.tensor.transpose(flipped[:, c, :], x_sb[b][:, m, c * P : (c + 1) * P], ident_bf[:])
+
+        def transpose_p(b, m, e, flipped):
+            nc.tensor.transpose(flipped[:, e, :], p_bf[b][m][:, e * P : (e + 1) * P], ident_bf[:])
+
+        def regroup_p(piece, b, m, flipped):
+            copy_out(piece, p_grouped[b][:, m, :, :], flipped[:].rearrange("s e r -> s r e"))
+
+        def quantise_p(b, m):
+            nc.vector.quantize_mx(
+                out=p_codes[b][:, m, :].bitcast(FP8X4),
+                scales=p_scales[b][:, m, :],
+                in_=p_grouped[b][:, m, :, :].rearrange("s r e -> s (r e)"),
+            )
+
+        def h_bank(n):
+            return n // (2 * EXPERTS), (n // 2) % EXPERTS, n % 2
+
+        def new_flipped_words():
+            return psum.tile([P, 2, 2, P], F32, tag="small", name="flipped_words")
+
+        def transpose_h(n, c, flipped):
+            b, e, half = h_bank(n)
+            gg, u = c // 2, c % 2
+            g = 2 * half + gg
+            nc.tensor.transpose(
+                flipped[:, gg, u, :],
+                h_sb[b][e][:].bitcast(F32)[:, PASS_WORDS * g + u : PASS_WORDS * (g + 1) : 2],
+                ident_f32[:],
+            )
+
+        def quantise_h(b, e):
+            nc.vector.quantize_mx(
+                out=h_codes[b][e][:].rearrange("r g s -> r (g s)").bitcast(FP8X4),
+                scales=h_scales[b][e][:].rearrange("r g s -> r (g s)"),
+                in_=h_grouped[(b, e)][:].rearrange("r g s t -> r (g s t)"),
+            )
+
+        def regroup_h(n, flipped):
+            b, e, half = h_bank(n)
+            if half == 0:
+                h_grouped[(b, e)] = stage.tile([P, PASSES, P, PACK], BF16, name="h_grouped", align_bytes=64)
+            copy_out(
+                0 if n % 4 == 3 else 1,
+                h_grouped[(b, e)][:, 2 * half : 2 * half + 2, :, :].bitcast(F32),
+                flipped[:].rearrange("r g u s -> r g s u"),
+            )
+            if half == 0 and n > 0:
+                quantise_h(*h_bank(n - 1)[0:2])
+
+        for e in range(EXPERTS):
+            flipped = new_flipped_bf16()
             for c in range(FEAT_BLOCKS):
-                nc.tensor.transpose(flipped[:, c, :], phi_sb[e][:, c * P : (c + 1) * P], ident_bf[:])
+                transpose_phi(e, c, flipped)
             copy_out(e, phiT[:, :, e * P : (e + 1) * P], flipped[:])
-
-        def transpose_x(b, m):
-            flipped = psum.tile([P, FEAT_BLOCKS, P], BF16, tag="small", name="x_flipped")
+        for m in range(TOKEN_TILES):
+            flipped = new_flipped_bf16()
             for c in range(FEAT_BLOCKS):
-                nc.tensor.transpose(flipped[:, c, :], x_sb[b][:, m, c * P : (c + 1) * P], ident_bf[:])
-            copy_out(m, xT[b][:, m, :, :], flipped[:])
+                transpose_x(0, m, c, flipped)
+            copy_out(m, xT[0][:, m, :, :], flipped[:])
 
-        def softmax_numerator(b, m):
-            col = b * TOKEN_TILES + m
+        token_tiles = [(b, m) for b in range(BATCH) for m in range(TOKEN_TILES)]
+        for i, (b, m) in enumerate(token_tiles):
             logits = psum.tile([P, ALL_SLOTS], F32, tag="wide", name="logits")
+            flipped = new_flipped_bf16()
+            if i > 0:
+                flipped_words = new_flipped_words()
             for c in range(FEAT_BLOCKS):
                 nc.tensor.matmul(
                     out=logits[:], lhsT=xT[b][:, m, c, :], rhs=phiT[:, c, :],
                     start=(c == 0), stop=(c == FEAT_BLOCKS - 1),
                 )
+                if b == 0:
+                    transpose_x(1, m, c, flipped)
+                else:
+                    transpose_p(0, m, c, flipped)
+                if i > 0:
+                    transpose_h(i - 1, c, flipped_words)
+            if i > 0:
+                regroup_h(i - 1, flipped_words)
             nc.vector.tensor_reduce(
-                out=neg_max[:, col : col + 1], in_=logits[:], axis=AXIS.X, op=ALU.max, negate=True
+                out=neg_max[:, i : i + 1], in_=logits[:], axis=AXIS.X, op=ALU.max, negate=True
             )
             nc.scalar.activation(
                 out=p_bf[b][m][:], in_=logits[:], func=ACT.Exp,
-                bias=neg_max[:, col : col + 1], scale=1.0, accum_out=p_sum[:, col : col + 1],
+                bias=neg_max[:, i : i + 1], scale=1.0, accum_out=p_sum[:, i : i + 1],
             )
+            if b == 0:
+                nc.vector.tensor_copy(out=xT[1][:, m, :, :], in_=flipped[:])
+            else:
+                regroup_p(0, 0, m, flipped)
+                if m > 0:
+                    quantise_p(0, m - 1)
+        quantise_p(0, TOKEN_TILES - 1)
 
-        for e in range(EXPERTS):
-            transpose_phi(e)
-        for b in range(BATCH):
-            for m in range(TOKEN_TILES):
-                transpose_x(b, m)
-            for m in range(TOKEN_TILES):
-                softmax_numerator(b, m)
+        for n in range(len(token_tiles) - 1, 2 * BATCH * EXPERTS):
+            flipped_words = new_flipped_words()
+            for c in range(4):
+                transpose_h(n, c, flipped_words)
+            regroup_h(n, flipped_words)
+        quantise_h(BATCH - 1, EXPERTS - 1)
+        for m in range(TOKEN_TILES):
+            flipped = new_flipped_bf16()
+            for e in range(EXPERTS):
+                transpose_p(1, m, e, flipped)
+            regroup_p(m, 1, m, flipped)
+            if m > 0:
+                quantise_p(1, m - 1)
+        quantise_p(1, TOKEN_TILES - 1)
+        nc.vector.reciprocal(out=inv_sum[:], in_=p_sum[:])
 
         bias_sb = keep.tile([P, FEAT_BLOCKS, P, EXPERTS], F32, name="bias_sb")
         for j in range(FEAT_BLOCKS):
@@ -136,70 +224,6 @@ def tile_mixtureexpertsmlp_pb_e_kernel(tc, h, w2_words, w2_scales, b2, x, phi, o
                     out=spread[:, e, :], lhsT=ones_bf[:], rhs=b2_row[:, first : first + P], start=True, stop=True
                 )
             copy_out(j, bias_sb[:, j, :, :], spread[:].rearrange("s e d -> s d e"))
-
-        p_grouped = [keep.tile([P, TOKEN_TILES, P, PACK], BF16, name="p_grouped%d" % b, align_bytes=64) for b in range(BATCH)]
-        p_codes = [keep.tile([P, TOKEN_TILES, P], U32, name="p_codes%d" % b, align_bytes=64) for b in range(BATCH)]
-        p_scales = [keep.tile([P, TOKEN_TILES, P], U8, name="p_scales%d" % b, align_bytes=64) for b in range(BATCH)]
-
-        def transpose_p(b, m):
-            flipped = psum.tile([P, EXPERTS, P], BF16, tag="small", name="p_flipped")
-            for e in range(EXPERTS):
-                nc.tensor.transpose(flipped[:, e, :], p_bf[b][m][:, e * P : (e + 1) * P], ident_bf[:])
-            copy_out(m, p_grouped[b][:, m, :, :], flipped[:].rearrange("s e r -> s r e"))
-
-        def quantise_p(b, m):
-            nc.vector.quantize_mx(
-                out=p_codes[b][:, m, :].bitcast(FP8X4),
-                scales=p_scales[b][:, m, :],
-                in_=p_grouped[b][:, m, :, :].rearrange("s r e -> s (r e)"),
-            )
-
-        token_tiles = [(b, m) for b in range(BATCH) for m in range(TOKEN_TILES)]
-        for i, (b, m) in enumerate(token_tiles):
-            transpose_p(b, m)
-            if i > 0:
-                quantise_p(*token_tiles[i - 1])
-        quantise_p(*token_tiles[-1])
-        nc.vector.reciprocal(out=inv_sum[:], in_=p_sum[:])
-
-        h_codes = [[keep.tile([P, PASSES, P], U32, name="h_codes%d_%d" % (b, e), align_bytes=64) for e in range(EXPERTS)] for b in range(BATCH)]
-        h_scales = [[keep.tile([P, PASSES, P], U8, name="h_scales%d_%d" % (b, e), align_bytes=64) for e in range(EXPERTS)] for b in range(BATCH)]
-
-        def transpose_h(b, e):
-            words = h_sb[b][e][:].bitcast(F32)
-            grouped = stage.tile([P, PASSES, P, PACK], BF16, name="h_grouped", align_bytes=64)
-            for half in range(2):
-                flipped = psum.tile([P, 2, 2, P], F32, tag="small", name="h_flipped")
-                for gg in range(2):
-                    g = 2 * half + gg
-                    for u in range(2):
-                        nc.tensor.transpose(
-                            flipped[:, gg, u, :],
-                            words[:, PASS_WORDS * g + u : PASS_WORDS * (g + 1) : 2],
-                            ident_f32[:],
-                        )
-                copy_out(
-                    0 if (half == 1 and e % 2 == 1) else 1,
-                    grouped[:, 2 * half : 2 * half + 2, :, :].bitcast(F32),
-                    flipped[:].rearrange("r g u s -> r g s u"),
-                )
-            return grouped
-
-        def quantise_h(b, e, grouped):
-            nc.vector.quantize_mx(
-                out=h_codes[b][e][:].rearrange("r g s -> r (g s)").bitcast(FP8X4),
-                scales=h_scales[b][e][:].rearrange("r g s -> r (g s)"),
-                in_=grouped[:].rearrange("r g s t -> r (g s t)"),
-            )
-
-        waiting = None
-        for b in range(BATCH):
-            for e in range(EXPERTS):
-                grouped = transpose_h(b, e)
-                if waiting is not None:
-                    quantise_h(*waiting)
-                waiting = (b, e, grouped)
-        quantise_h(*waiting)
 
         y_codes = [keep.tile([P, P], U32, name="y_codes%d" % i, align_bytes=64) for i in range(BATCH * FEAT_BLOCKS)]
         y_scales = [keep.tile([P, P], U8, name="y_scales%d" % i, align_bytes=64) for i in range(BATCH * FEAT_BLOCKS)]

@@ -23,8 +23,8 @@ ALL_SLOTS = EXPERTS * SLOTS
 TOKEN_TILES = TOKENS // P
 FEAT_BLOCKS = FEAT // P
 PASSES = HIDDEN // K_PASS
-WORDS = HIDDEN // 2
 PASS_WORDS = K_PASS // 2
+H_BANKS = 2 * EXPERTS
 
 COMBINE_LAG = 2
 
@@ -37,7 +37,6 @@ def tile_mixtureexpertsmlp_pb_e_kernel(tc, h, w2_words, w2_scales, b2, x, phi, o
         ctx.enter_context(tc.manual_schedule())
         keep = ctx.enter_context(tc.tile_pool(name="keep", bufs=1))
         stage = ctx.enter_context(tc.tile_pool(name="stage", bufs=3))
-        results = ctx.enter_context(tc.tile_pool(name="results", bufs=TOKEN_TILES))
         psum = ctx.enter_context(tc.psum_pool(name="psum", bufs=4))
 
         def copy_out(piece, out_ap, in_ap):
@@ -46,43 +45,42 @@ def tile_mixtureexpertsmlp_pb_e_kernel(tc, h, w2_words, w2_scales, b2, x, phi, o
             else:
                 nc.scalar.copy(out=out_ap, in_=in_ap)
 
+        b2_row = keep.tile([P, EXPERTS * FEAT], BF16, name="b2_row")
+        nc.vector.memset(b2_row[:].bitcast(I32), 0)
+        ones_bf = keep.tile([P, P], BF16, name="ones_bf")
+        nc.vector.memset(ones_bf[:], 1.0)
+        warm = keep.tile([P, 1], F32, name="warm")
+        nc.vector.memset(warm[:], 0.0)
+        nc.scalar.activation(out=warm[:], in_=warm[:], func=ACT.Exp)
         ident_bf = keep.tile([P, P], BF16, name="ident_bf")
         ident_f32 = keep.tile([P, P], F32, name="ident_f32")
         make_identity(nc, ident_bf[:])
         make_identity(nc, ident_f32[:])
-        ones_bf = keep.tile([P, P], BF16, name="ones_bf")
-        nc.vector.memset(ones_bf[:], 1.0)
-        b2_row = keep.tile([P, EXPERTS * FEAT], BF16, name="b2_row")
-        nc.vector.memset(b2_row[:].bitcast(I32), 0)
         w_scales = keep.tile([P, EXPERTS * PASSES, FEAT], U8, name="w_scales", align_bytes=64)
         nc.vector.memset(w_scales[:].rearrange("r g n -> r (g n)").bitcast(I32), 0)
-        warm = keep.tile([P, 1], F32, name="warm")
-        nc.vector.memset(warm[:], 0.0)
-        nc.scalar.activation(out=warm[:], in_=warm[:], func=ACT.Exp)
 
         phi_sb = [keep.tile([P, FEAT], BF16, name="phi_sb%d" % e) for e in range(EXPERTS)]
+        x_sb = [keep.tile([P, TOKEN_TILES, FEAT], BF16, name="x_sb%d" % b) for b in range(BATCH)]
+        h_sb = [[keep.tile([P, HIDDEN], BF16, name="h_sb%d_%d" % (b, e)) for e in range(EXPERTS)] for b in range(BATCH)]
+        w_codes = [keep.tile([P, PASSES, FEAT], U32, name="w_codes%d" % e, align_bytes=64) for e in range(EXPERTS)]
         for e in range(EXPERTS):
             nc.sync.dma_start(out=phi_sb[e][:], in_=phi[e])
-        x_sb = [keep.tile([P, TOKEN_TILES, FEAT], BF16, name="x_sb%d" % b) for b in range(BATCH)]
+        nc.sync.dma_start(out=b2_row[0:1, :], in_=b2.rearrange("(o e) d -> o (e d)", o=1))
         for b in range(BATCH):
             nc.sync.dma_start(out=x_sb[b][:], in_=x[b].rearrange("(r m) d -> r m d", m=TOKEN_TILES))
-        nc.sync.dma_start(out=b2_row[0:1, :], in_=b2.rearrange("(o e) d -> o (e d)", o=1))
-        h_sb = [[keep.tile([P, HIDDEN], BF16, name="h_sb%d_%d" % (b, e)) for e in range(EXPERTS)] for b in range(BATCH)]
-        for b in range(BATCH):
-            for e in range(EXPERTS):
-                nc.sync.dma_start(out=h_sb[b][e][:], in_=h[b, e])
-        for low_q in range(2):
-            for i in range(4):
-                nc.sync.dma_start(
-                    out=w_scales[32 * low_q + i : P : 64, :, :].bitcast(I32),
-                    in_=w2_scales[:, 4 * low_q + i : 16 : 8, :].rearrange("g q n -> q g n").bitcast(I32),
-                )
-        w_codes = [keep.tile([P, PASSES, FEAT], U32, name="w_codes%d" % e, align_bytes=64) for e in range(EXPERTS)]
+        for i in range(4):
+            nc.sync.dma_start(out=h_sb[0][i][:], in_=h[0, i])
+            nc.sync.dma_start(
+                out=w_scales[i : P : 32, :, :].bitcast(I32),
+                in_=w2_scales[:, i : 16 : 4, :].rearrange("g q n -> q g n").bitcast(I32),
+            )
         for e in range(EXPERTS):
             nc.sync.dma_start(
                 out=w_codes[e][:].bitcast(I32),
                 in_=w2_words[PASSES * e : PASSES * (e + 1)].rearrange("g r n t -> r g (n t)").bitcast(I32),
             )
+        for e in range(EXPERTS):
+            nc.sync.dma_start(out=h_sb[1][e][:], in_=h[1, e])
 
         phiT = keep.tile([P, FEAT_BLOCKS, ALL_SLOTS], BF16, name="phiT")
         xT = [keep.tile([P, TOKEN_TILES, FEAT_BLOCKS, P], BF16, name="xT%d" % b) for b in range(BATCH)]
@@ -96,6 +94,9 @@ def tile_mixtureexpertsmlp_pb_e_kernel(tc, h, w2_words, w2_scales, b2, x, phi, o
         h_grouped = {}
         h_codes = [[keep.tile([P, PASSES, P], U32, name="h_codes%d_%d" % (b, e), align_bytes=64) for e in range(EXPERTS)] for b in range(BATCH)]
         h_scales = [[keep.tile([P, PASSES, P], U8, name="h_scales%d_%d" % (b, e), align_bytes=64) for e in range(EXPERTS)] for b in range(BATCH)]
+        bias_sb = keep.tile([P, FEAT_BLOCKS, P, EXPERTS], F32, name="bias_sb")
+        y_codes = [[keep.tile([P, P], U32, name="y_codes%d_%d" % (b, j), align_bytes=64) for j in range(FEAT_BLOCKS)] for b in range(BATCH)]
+        y_scales = [[keep.tile([P, P], U8, name="y_scales%d_%d" % (b, j), align_bytes=64) for j in range(FEAT_BLOCKS)] for b in range(BATCH)]
 
         def new_flipped_bf16():
             return psum.tile([P, 4, P], BF16, tag="small", name="flipped_bf16")
@@ -119,19 +120,15 @@ def tile_mixtureexpertsmlp_pb_e_kernel(tc, h, w2_words, w2_scales, b2, x, phi, o
                 in_=p_grouped[b][:, m, :, :].rearrange("s r e -> s (r e)"),
             )
 
-        def h_bank(n):
-            return n // (2 * EXPERTS), (n // 2) % EXPERTS, n % 2
-
         def new_flipped_words():
             return psum.tile([P, 2, 2, P], F32, tag="small", name="flipped_words")
 
-        def transpose_h(n, c, flipped):
-            b, e, half = h_bank(n)
+        def transpose_h(b, n, c, flipped):
             gg, u = c // 2, c % 2
-            g = 2 * half + gg
+            g = 2 * (n % 2) + gg
             nc.tensor.transpose(
                 flipped[:, gg, u, :],
-                h_sb[b][e][:].bitcast(F32)[:, PASS_WORDS * g + u : PASS_WORDS * (g + 1) : 2],
+                h_sb[b][n // 2][:].bitcast(F32)[:, PASS_WORDS * g + u : PASS_WORDS * (g + 1) : 2],
                 ident_f32[:],
             )
 
@@ -139,26 +136,88 @@ def tile_mixtureexpertsmlp_pb_e_kernel(tc, h, w2_words, w2_scales, b2, x, phi, o
             nc.vector.quantize_mx(
                 out=h_codes[b][e][:].rearrange("r g s -> r (g s)").bitcast(FP8X4),
                 scales=h_scales[b][e][:].rearrange("r g s -> r (g s)"),
-                in_=h_grouped[(b, e)][:].rearrange("r g s t -> r (g s t)"),
+                in_=h_grouped[e][:].rearrange("r g s t -> r (g s t)"),
             )
 
-        def regroup_h(n, flipped):
-            b, e, half = h_bank(n)
+        def regroup_h(piece, b, n, flipped):
+            e, half = n // 2, n % 2
             if half == 0:
-                h_grouped[(b, e)] = stage.tile([P, PASSES, P, PACK], BF16, name="h_grouped", align_bytes=64)
+                h_grouped[e] = stage.tile([P, PASSES, P, PACK], BF16, name="h_grouped", align_bytes=64)
             copy_out(
-                0 if n % 4 == 3 else 1,
-                h_grouped[(b, e)][:, 2 * half : 2 * half + 2, :, :].bitcast(F32),
+                piece,
+                h_grouped[e][:, 2 * half : 2 * half + 2, :, :].bitcast(F32),
                 flipped[:].rearrange("r g u s -> r g s u"),
             )
-            if half == 0 and n > 0:
-                quantise_h(*h_bank(n - 1)[0:2])
+            if half == 0 and e > 0:
+                quantise_h(b, e - 1)
+
+        def first_layer(b, j):
+            cols = slice(j * P, (j + 1) * P)
+            y_psum = psum.tile([P, EXPERTS, P], F32, tag="small", name="y_psum")
+            for e in range(EXPERTS):
+                for g in range(PASSES):
+                    nc.tensor.matmul_mx(
+                        out=y_psum[:, e, :],
+                        lhsT=h_codes[b][e][:, g, :].bitcast(FP8X4),
+                        lhsT_scale=h_scales[b][e][:, g, :],
+                        rhs=w_codes[e][:, g, cols].bitcast(FP8X4),
+                        rhs_scale=w_scales[:, e * PASSES + g, cols],
+                        start=(g == 0),
+                        stop=(g == PASSES - 1),
+                    )
+            y_grouped = stage.tile([P, P, PACK], BF16, name="y_grouped", align_bytes=64)
+            nc.vector.tensor_tensor(
+                out=y_grouped[:], in0=y_psum[:].rearrange("s e d -> s d e"), in1=bias_sb[:, j, :, :], op=ALU.add
+            )
+            nc.vector.quantize_mx(
+                out=y_codes[b][j][:].bitcast(FP8X4),
+                scales=y_scales[b][j][:],
+                in_=y_grouped[:].rearrange("s d e -> s (d e)"),
+            )
+
+        def combine(b, j):
+            result = stage.tile([P, TOKEN_TILES, P], F32, name="result")
+            for half in range(2):
+                combined = psum.tile([P, 2, P], F32, tag="wide", name="combined")
+                for mm in range(2):
+                    m = 2 * half + mm
+                    nc.tensor.matmul_mx(
+                        out=combined[:, mm, :],
+                        lhsT=p_codes[b][:, m, :].bitcast(FP8X4),
+                        lhsT_scale=p_scales[b][:, m, :],
+                        rhs=y_codes[b][j][:].bitcast(FP8X4),
+                        rhs_scale=y_scales[b][j][:],
+                        start=True,
+                        stop=True,
+                    )
+                for mm in range(2):
+                    m = 2 * half + mm
+                    col = b * TOKEN_TILES + m
+                    if half == 0:
+                        nc.scalar.activation(
+                            out=result[:, m, :], in_=combined[:, mm, :], func=ACT.Copy, scale=inv_sum[:, col : col + 1]
+                        )
+                    else:
+                        nc.vector.tensor_scalar_mul(
+                            out=result[:, m, :], in0=combined[:, mm, :], scalar1=inv_sum[:, col : col + 1]
+                        )
+            nc.sync.dma_start(
+                out=out[b].rearrange("(r m) d -> r m d", m=TOKEN_TILES)[:, :, j * P : (j + 1) * P], in_=result[:]
+            )
 
         for e in range(EXPERTS):
             flipped = new_flipped_bf16()
             for c in range(FEAT_BLOCKS):
                 transpose_phi(e, c, flipped)
             copy_out(e, phiT[:, :, e * P : (e + 1) * P], flipped[:])
+        for j in range(FEAT_BLOCKS):
+            spread = psum.tile([P, EXPERTS, P], F32, tag="small", name="bias_spread")
+            for e in range(EXPERTS):
+                first = e * FEAT + j * P
+                nc.tensor.matmul(
+                    out=spread[:, e, :], lhsT=ones_bf[:], rhs=b2_row[:, first : first + P], start=True, stop=True
+                )
+            copy_out(j, bias_sb[:, j, :, :], spread[:].rearrange("s e d -> s d e"))
         for m in range(TOKEN_TILES):
             flipped = new_flipped_bf16()
             for c in range(FEAT_BLOCKS):
@@ -181,9 +240,9 @@ def tile_mixtureexpertsmlp_pb_e_kernel(tc, h, w2_words, w2_scales, b2, x, phi, o
                 else:
                     transpose_p(0, m, c, flipped)
                 if i > 0:
-                    transpose_h(i - 1, c, flipped_words)
+                    transpose_h(0, i - 1, c, flipped_words)
             if i > 0:
-                regroup_h(i - 1, flipped_words)
+                regroup_h(1, 0, i - 1, flipped_words)
             nc.vector.tensor_reduce(
                 out=neg_max[:, i : i + 1], in_=logits[:], axis=AXIS.X, op=ALU.max, negate=True
             )
@@ -192,97 +251,40 @@ def tile_mixtureexpertsmlp_pb_e_kernel(tc, h, w2_words, w2_scales, b2, x, phi, o
                 bias=neg_max[:, i : i + 1], scale=1.0, accum_out=p_sum[:, i : i + 1],
             )
             if b == 0:
-                nc.vector.tensor_copy(out=xT[1][:, m, :, :], in_=flipped[:])
+                copy_out(m, xT[1][:, m, :, :], flipped[:])
             else:
                 regroup_p(0, 0, m, flipped)
                 if m > 0:
                     quantise_p(0, m - 1)
+        flipped_words = new_flipped_words()
+        for c in range(4):
+            transpose_h(0, H_BANKS - 1, c, flipped_words)
+        regroup_h(1, 0, H_BANKS - 1, flipped_words)
         quantise_p(0, TOKEN_TILES - 1)
-
-        for n in range(len(token_tiles) - 1, 2 * BATCH * EXPERTS):
-            flipped_words = new_flipped_words()
-            for c in range(4):
-                transpose_h(n, c, flipped_words)
-            regroup_h(n, flipped_words)
-        quantise_h(BATCH - 1, EXPERTS - 1)
-        for m in range(TOKEN_TILES):
-            flipped = new_flipped_bf16()
-            for e in range(EXPERTS):
-                transpose_p(1, m, e, flipped)
-            regroup_p(m, 1, m, flipped)
-            if m > 0:
-                quantise_p(1, m - 1)
-        quantise_p(1, TOKEN_TILES - 1)
+        quantise_h(0, EXPERTS - 1)
         nc.vector.reciprocal(out=inv_sum[:], in_=p_sum[:])
 
-        bias_sb = keep.tile([P, FEAT_BLOCKS, P, EXPERTS], F32, name="bias_sb")
-        for j in range(FEAT_BLOCKS):
-            spread = psum.tile([P, EXPERTS, P], F32, tag="small", name="bias_spread")
-            for e in range(EXPERTS):
-                first = e * FEAT + j * P
-                nc.tensor.matmul(
-                    out=spread[:, e, :], lhsT=ones_bf[:], rhs=b2_row[:, first : first + P], start=True, stop=True
-                )
-            copy_out(j, bias_sb[:, j, :, :], spread[:].rearrange("s e d -> s d e"))
-
-        y_codes = [keep.tile([P, P], U32, name="y_codes%d" % i, align_bytes=64) for i in range(BATCH * FEAT_BLOCKS)]
-        y_scales = [keep.tile([P, P], U8, name="y_scales%d" % i, align_bytes=64) for i in range(BATCH * FEAT_BLOCKS)]
-        combined = {}
-
-        def first_layer(b, j):
-            cols = slice(j * P, (j + 1) * P)
-            y_psum = psum.tile([P, EXPERTS, P], F32, tag="small", name="y_psum")
-            for e in range(EXPERTS):
-                for g in range(PASSES):
-                    nc.tensor.matmul_mx(
-                        out=y_psum[:, e, :],
-                        lhsT=h_codes[b][e][:, g, :].bitcast(FP8X4),
-                        lhsT_scale=h_scales[b][e][:, g, :],
-                        rhs=w_codes[e][:, g, cols].bitcast(FP8X4),
-                        rhs_scale=w_scales[:, e * PASSES + g, cols],
-                        start=(g == 0),
-                        stop=(g == PASSES - 1),
-                    )
-            y_grouped = stage.tile([P, P, PACK], BF16, name="y_grouped", align_bytes=64)
-            nc.vector.tensor_tensor(
-                out=y_grouped[:], in0=y_psum[:].rearrange("s e d -> s d e"), in1=bias_sb[:, j, :, :], op=ALU.add
-            )
-            nc.vector.quantize_mx(
-                out=y_codes[b * FEAT_BLOCKS + j][:].bitcast(FP8X4),
-                scales=y_scales[b * FEAT_BLOCKS + j][:],
-                in_=y_grouped[:].rearrange("s d e -> s (d e)"),
-            )
-
-        def combine(b, j):
+        def prepare_second_batch():
+            for n in range(H_BANKS):
+                flipped_words = new_flipped_words()
+                for c in range(4):
+                    transpose_h(1, n, c, flipped_words)
+                regroup_h(0 if n % 4 == 3 else 1, 1, n, flipped_words)
+            quantise_h(1, EXPERTS - 1)
             for m in range(TOKEN_TILES):
-                if j == 0:
-                    combined[m] = psum.tile([P, FEAT], F32, tag="wide", name="combined")
-                nc.tensor.matmul_mx(
-                    out=combined[m][:, j * P : (j + 1) * P],
-                    lhsT=p_codes[b][:, m, :].bitcast(FP8X4),
-                    lhsT_scale=p_scales[b][:, m, :],
-                    rhs=y_codes[b * FEAT_BLOCKS + j][:].bitcast(FP8X4),
-                    rhs_scale=y_scales[b * FEAT_BLOCKS + j][:],
-                    start=True,
-                    stop=True,
-                )
-
-        def divide_and_store(b, m):
-            col = b * TOKEN_TILES + m
-            result = results.tile([P, FEAT], F32, name="result")
-            if m % 2 == 0:
-                nc.scalar.activation(out=result[:], in_=combined[m][:], func=ACT.Copy, scale=inv_sum[:, col : col + 1])
-            else:
-                nc.vector.tensor_scalar_mul(out=result[:], in0=combined[m][:], scalar1=inv_sum[:, col : col + 1])
-            nc.sync.dma_start(out=out[b].rearrange("(r m) d -> r m d", m=TOKEN_TILES)[:, m, :], in_=result[:])
+                flipped = new_flipped_bf16()
+                for e in range(EXPERTS):
+                    transpose_p(1, m, e, flipped)
+                regroup_p(m, 1, m, flipped)
+                if m > 0:
+                    quantise_p(1, m - 1)
+            quantise_p(1, TOKEN_TILES - 1)
 
         blocks = [(b, j) for b in range(BATCH) for j in range(FEAT_BLOCKS)]
         for i in range(len(blocks) + COMBINE_LAG):
             if i < len(blocks):
+                if blocks[i] == (1, 0):
+                    prepare_second_batch()
                 first_layer(*blocks[i])
             if i >= COMBINE_LAG:
-                b, j = blocks[i - COMBINE_LAG]
-                combine(b, j)
-                if j == FEAT_BLOCKS - 1:
-                    for m in range(TOKEN_TILES):
-                        divide_and_store(b, m)
+                combine(*blocks[i - COMBINE_LAG])

@@ -24,7 +24,6 @@ TOKEN_TILES = TOKENS // P
 FEAT_BLOCKS = FEAT // P
 PASSES = HIDDEN // K_PASS
 PASS_WORDS = K_PASS // 2
-H_BANKS = 2 * EXPERTS
 
 COMBINE_LAG = 2
 
@@ -37,7 +36,8 @@ def tile_mixtureexpertsmlp_pb_e_kernel(tc, h, w2_words, w2_scales, b2, x, phi, o
         ctx.enter_context(tc.manual_schedule())
         keep = ctx.enter_context(tc.tile_pool(name="keep", bufs=1))
         stage = ctx.enter_context(tc.tile_pool(name="stage", bufs=3))
-        psum = ctx.enter_context(tc.psum_pool(name="psum", bufs=4))
+        psum_small = ctx.enter_context(tc.psum_pool(name="psum_small", bufs=5))
+        psum_wide = ctx.enter_context(tc.psum_pool(name="psum_wide", bufs=3))
 
         def copy_out(piece, out_ap, in_ap):
             if piece % 2 == 0:
@@ -65,11 +65,13 @@ def tile_mixtureexpertsmlp_pb_e_kernel(tc, h, w2_words, w2_scales, b2, x, phi, o
         w_codes = [keep.tile([P, PASSES, FEAT], U32, name="w_codes%d" % e, align_bytes=64) for e in range(EXPERTS)]
         for e in range(EXPERTS):
             nc.sync.dma_start(out=phi_sb[e][:], in_=phi[e])
-        nc.sync.dma_start(out=b2_row[0:1, :], in_=b2.rearrange("(o e) d -> o (e d)", o=1))
         for b in range(BATCH):
             nc.sync.dma_start(out=x_sb[b][:], in_=x[b].rearrange("(r m) d -> r m d", m=TOKEN_TILES))
+        for e in range(EXPERTS):
+            nc.sync.dma_start(out=h_sb[0][e][:], in_=h[0, e])
+        nc.sync.dma_start(out=b2_row[0:1, :], in_=b2.rearrange("(o e) d -> o (e d)", o=1))
         for i in range(4):
-            nc.sync.dma_start(out=h_sb[0][i][:], in_=h[0, i])
+            nc.sync.dma_start(out=h_sb[1][i][:], in_=h[1, i])
             nc.sync.dma_start(
                 out=w_scales[i : P : 32, :, :].bitcast(I32),
                 in_=w2_scales[:, i : 16 : 4, :].rearrange("g q n -> q g n").bitcast(I32),
@@ -79,8 +81,6 @@ def tile_mixtureexpertsmlp_pb_e_kernel(tc, h, w2_words, w2_scales, b2, x, phi, o
                 out=w_codes[e][:].bitcast(I32),
                 in_=w2_words[PASSES * e : PASSES * (e + 1)].rearrange("g r n t -> r g (n t)").bitcast(I32),
             )
-        for e in range(EXPERTS):
-            nc.sync.dma_start(out=h_sb[1][e][:], in_=h[1, e])
 
         phiT = keep.tile([P, FEAT_BLOCKS, ALL_SLOTS], BF16, name="phiT")
         xT = [keep.tile([P, TOKEN_TILES, FEAT_BLOCKS, P], BF16, name="xT%d" % b) for b in range(BATCH)]
@@ -91,7 +91,6 @@ def tile_mixtureexpertsmlp_pb_e_kernel(tc, h, w2_words, w2_scales, b2, x, phi, o
         p_grouped = [keep.tile([P, TOKEN_TILES, P, PACK], BF16, name="p_grouped%d" % b, align_bytes=64) for b in range(BATCH)]
         p_codes = [keep.tile([P, TOKEN_TILES, P], U32, name="p_codes%d" % b, align_bytes=64) for b in range(BATCH)]
         p_scales = [keep.tile([P, TOKEN_TILES, P], U8, name="p_scales%d" % b, align_bytes=64) for b in range(BATCH)]
-        h_grouped = {}
         h_codes = [[keep.tile([P, PASSES, P], U32, name="h_codes%d_%d" % (b, e), align_bytes=64) for e in range(EXPERTS)] for b in range(BATCH)]
         h_scales = [[keep.tile([P, PASSES, P], U8, name="h_scales%d_%d" % (b, e), align_bytes=64) for e in range(EXPERTS)] for b in range(BATCH)]
         bias_sb = keep.tile([P, FEAT_BLOCKS, P, EXPERTS], F32, name="bias_sb")
@@ -99,7 +98,7 @@ def tile_mixtureexpertsmlp_pb_e_kernel(tc, h, w2_words, w2_scales, b2, x, phi, o
         y_scales = [[keep.tile([P, P], U8, name="y_scales%d_%d" % (b, j), align_bytes=64) for j in range(FEAT_BLOCKS)] for b in range(BATCH)]
 
         def new_flipped_bf16():
-            return psum.tile([P, 4, P], BF16, tag="small", name="flipped_bf16")
+            return psum_small.tile([P, 4, P], BF16, tag="small", name="flipped_bf16")
 
         def transpose_phi(e, c, flipped):
             nc.tensor.transpose(flipped[:, c, :], phi_sb[e][:, c * P : (c + 1) * P], ident_bf[:])
@@ -121,39 +120,31 @@ def tile_mixtureexpertsmlp_pb_e_kernel(tc, h, w2_words, w2_scales, b2, x, phi, o
             )
 
         def new_flipped_words():
-            return psum.tile([P, 2, 2, P], F32, tag="small", name="flipped_words")
+            return psum_small.tile([P, 2, 2, P], F32, tag="small", name="flipped_words")
 
-        def transpose_h(b, n, c, flipped):
-            gg, u = c // 2, c % 2
-            g = 2 * (n % 2) + gg
+        def transpose_h(b, e, g, u, flipped):
             nc.tensor.transpose(
-                flipped[:, gg, u, :],
-                h_sb[b][n // 2][:].bitcast(F32)[:, PASS_WORDS * g + u : PASS_WORDS * (g + 1) : 2],
+                flipped[:, g % 2, u, :],
+                h_sb[b][e][:].bitcast(F32)[:, PASS_WORDS * g + u : PASS_WORDS * (g + 1) : 2],
                 ident_f32[:],
             )
 
-        def quantise_h(b, e):
+        def regroup_h(half, grouped, flipped):
+            nc.scalar.copy(
+                out=grouped[:, 2 * half : 2 * half + 2, :, :].bitcast(F32),
+                in_=flipped[:].rearrange("r g u s -> r g s u"),
+            )
+
+        def quantise_h(b, e, grouped):
             nc.vector.quantize_mx(
                 out=h_codes[b][e][:].rearrange("r g s -> r (g s)").bitcast(FP8X4),
                 scales=h_scales[b][e][:].rearrange("r g s -> r (g s)"),
-                in_=h_grouped[e][:].rearrange("r g s t -> r (g s t)"),
+                in_=grouped[:].rearrange("r g s t -> r (g s t)"),
             )
-
-        def regroup_h(piece, b, n, flipped):
-            e, half = n // 2, n % 2
-            if half == 0:
-                h_grouped[e] = stage.tile([P, PASSES, P, PACK], BF16, name="h_grouped", align_bytes=64)
-            copy_out(
-                piece,
-                h_grouped[e][:, 2 * half : 2 * half + 2, :, :].bitcast(F32),
-                flipped[:].rearrange("r g u s -> r g s u"),
-            )
-            if half == 0 and e > 0:
-                quantise_h(b, e - 1)
 
         def first_layer(b, j):
             cols = slice(j * P, (j + 1) * P)
-            y_psum = psum.tile([P, EXPERTS, P], F32, tag="small", name="y_psum")
+            y_psum = psum_small.tile([P, EXPERTS, P], F32, tag="small", name="y_psum")
             for e in range(EXPERTS):
                 for g in range(PASSES):
                     nc.tensor.matmul_mx(
@@ -175,10 +166,10 @@ def tile_mixtureexpertsmlp_pb_e_kernel(tc, h, w2_words, w2_scales, b2, x, phi, o
                 in_=y_grouped[:].rearrange("s d e -> s (d e)"),
             )
 
-        def combine(b, j):
+        def combine(b, j, vector_helps):
             result = stage.tile([P, TOKEN_TILES, P], F32, name="result")
             for half in range(2):
-                combined = psum.tile([P, 2, P], F32, tag="wide", name="combined")
+                combined = psum_wide.tile([P, 2, P], F32, tag="wide", name="combined")
                 for mm in range(2):
                     m = 2 * half + mm
                     nc.tensor.matmul_mx(
@@ -193,7 +184,7 @@ def tile_mixtureexpertsmlp_pb_e_kernel(tc, h, w2_words, w2_scales, b2, x, phi, o
                 for mm in range(2):
                     m = 2 * half + mm
                     col = b * TOKEN_TILES + m
-                    if half == 0:
+                    if half == 0 or not vector_helps:
                         nc.scalar.activation(
                             out=result[:, m, :], in_=combined[:, mm, :], func=ACT.Copy, scale=inv_sum[:, col : col + 1]
                         )
@@ -210,8 +201,54 @@ def tile_mixtureexpertsmlp_pb_e_kernel(tc, h, w2_words, w2_scales, b2, x, phi, o
             for c in range(FEAT_BLOCKS):
                 transpose_phi(e, c, flipped)
             copy_out(e, phiT[:, :, e * P : (e + 1) * P], flipped[:])
+        for m in range(TOKEN_TILES):
+            flipped = new_flipped_bf16()
+            for c in range(FEAT_BLOCKS):
+                transpose_x(0, m, c, flipped)
+            copy_out(m, xT[0][:, m, :, :], flipped[:])
+
+        waiting_h = None
+        for b in range(BATCH):
+            for m in range(TOKEN_TILES):
+                col = b * TOKEN_TILES + m
+                logits = psum_wide.tile([P, ALL_SLOTS], F32, tag="wide", name="logits")
+                flipped = new_flipped_bf16()
+                flipped_words = [new_flipped_words(), new_flipped_words()]
+                for c in range(FEAT_BLOCKS):
+                    nc.tensor.matmul(
+                        out=logits[:], lhsT=xT[b][:, m, c, :], rhs=phiT[:, c, :],
+                        start=(c == 0), stop=(c == FEAT_BLOCKS - 1),
+                    )
+                    if b == 0:
+                        transpose_x(1, m, c, flipped)
+                    else:
+                        transpose_p(0, m, c, flipped)
+                    for u in range(2):
+                        transpose_h(b, m, c, u, flipped_words[c // 2])
+                nc.vector.tensor_reduce(
+                    out=neg_max[:, col : col + 1], in_=logits[:], axis=AXIS.X, op=ALU.max, negate=True
+                )
+                h_grouped = stage.tile([P, PASSES, P, PACK], BF16, name="h_grouped", align_bytes=64)
+                for half in range(2):
+                    regroup_h(half, h_grouped, flipped_words[half])
+                nc.scalar.activation(
+                    out=p_bf[b][m][:], in_=logits[:], func=ACT.Exp,
+                    bias=neg_max[:, col : col + 1], scale=1.0, accum_out=p_sum[:, col : col + 1],
+                )
+                if b == 0:
+                    nc.vector.tensor_copy(out=xT[1][:, m, :, :], in_=flipped[:])
+                else:
+                    regroup_p(0, 0, m, flipped)
+                    if m > 0:
+                        quantise_p(0, m - 1)
+                if waiting_h is not None:
+                    quantise_h(*waiting_h)
+                waiting_h = (b, m, h_grouped)
+        quantise_p(0, TOKEN_TILES - 1)
+        quantise_h(*waiting_h)
+
         for j in range(FEAT_BLOCKS):
-            spread = psum.tile([P, EXPERTS, P], F32, tag="small", name="bias_spread")
+            spread = psum_small.tile([P, EXPERTS, P], F32, tag="small", name="bias_spread")
             for e in range(EXPERTS):
                 first = e * FEAT + j * P
                 nc.tensor.matmul(
@@ -220,71 +257,18 @@ def tile_mixtureexpertsmlp_pb_e_kernel(tc, h, w2_words, w2_scales, b2, x, phi, o
             copy_out(j, bias_sb[:, j, :, :], spread[:].rearrange("s e d -> s d e"))
         for m in range(TOKEN_TILES):
             flipped = new_flipped_bf16()
-            for c in range(FEAT_BLOCKS):
-                transpose_x(0, m, c, flipped)
-            copy_out(m, xT[0][:, m, :, :], flipped[:])
-
-        token_tiles = [(b, m) for b in range(BATCH) for m in range(TOKEN_TILES)]
-        for i, (b, m) in enumerate(token_tiles):
-            logits = psum.tile([P, ALL_SLOTS], F32, tag="wide", name="logits")
-            flipped = new_flipped_bf16()
-            if i > 0:
-                flipped_words = new_flipped_words()
-            for c in range(FEAT_BLOCKS):
-                nc.tensor.matmul(
-                    out=logits[:], lhsT=xT[b][:, m, c, :], rhs=phiT[:, c, :],
-                    start=(c == 0), stop=(c == FEAT_BLOCKS - 1),
-                )
-                if b == 0:
-                    transpose_x(1, m, c, flipped)
-                else:
-                    transpose_p(0, m, c, flipped)
-                if i > 0:
-                    transpose_h(0, i - 1, c, flipped_words)
-            if i > 0:
-                regroup_h(1, 0, i - 1, flipped_words)
-            nc.vector.tensor_reduce(
-                out=neg_max[:, i : i + 1], in_=logits[:], axis=AXIS.X, op=ALU.max, negate=True
-            )
-            nc.scalar.activation(
-                out=p_bf[b][m][:], in_=logits[:], func=ACT.Exp,
-                bias=neg_max[:, i : i + 1], scale=1.0, accum_out=p_sum[:, i : i + 1],
-            )
-            if b == 0:
-                copy_out(m, xT[1][:, m, :, :], flipped[:])
-            else:
-                regroup_p(0, 0, m, flipped)
-                if m > 0:
-                    quantise_p(0, m - 1)
-        flipped_words = new_flipped_words()
-        for c in range(4):
-            transpose_h(0, H_BANKS - 1, c, flipped_words)
-        regroup_h(1, 0, H_BANKS - 1, flipped_words)
-        quantise_p(0, TOKEN_TILES - 1)
-        quantise_h(0, EXPERTS - 1)
+            for e in range(EXPERTS):
+                transpose_p(1, m, e, flipped)
+            regroup_p(m, 1, m, flipped)
+            if m > 0:
+                quantise_p(1, m - 1)
+        quantise_p(1, TOKEN_TILES - 1)
         nc.vector.reciprocal(out=inv_sum[:], in_=p_sum[:])
-
-        def prepare_second_batch():
-            for n in range(H_BANKS):
-                flipped_words = new_flipped_words()
-                for c in range(4):
-                    transpose_h(1, n, c, flipped_words)
-                regroup_h(0 if n % 4 == 3 else 1, 1, n, flipped_words)
-            quantise_h(1, EXPERTS - 1)
-            for m in range(TOKEN_TILES):
-                flipped = new_flipped_bf16()
-                for e in range(EXPERTS):
-                    transpose_p(1, m, e, flipped)
-                regroup_p(m, 1, m, flipped)
-                if m > 0:
-                    quantise_p(1, m - 1)
-            quantise_p(1, TOKEN_TILES - 1)
 
         blocks = [(b, j) for b in range(BATCH) for j in range(FEAT_BLOCKS)]
         for i in range(len(blocks) + COMBINE_LAG):
             if i < len(blocks):
-                if blocks[i] == (1, 0):
-                    prepare_second_batch()
                 first_layer(*blocks[i])
             if i >= COMBINE_LAG:
-                combine(*blocks[i - COMBINE_LAG])
+                b, j = blocks[i - COMBINE_LAG]
+                combine(b, j, i >= len(blocks))

@@ -56,8 +56,8 @@ def tile_mixtureexpertsmlp_pb_e_kernel(tc, h, w2_words, w2_scales, b2, x, phi, o
         ident_f32 = keep.tile([P, P], F32, name="ident_f32")
         make_identity(nc, ident_bf[:])
         make_identity(nc, ident_f32[:])
-        w_scales = keep.tile([P, EXPERTS * PASSES, FEAT], U8, name="w_scales", align_bytes=64)
-        nc.vector.memset(w_scales[:].rearrange("r g n -> r (g n)").bitcast(I32), 0)
+        w_scales = keep.tile([P, EXPERTS, FEAT], U8, name="w_scales", align_bytes=64)
+        nc.vector.memset(w_scales[:].rearrange("r e n -> r (e n)").bitcast(I32), 0)
 
         phi_sb = [keep.tile([P, FEAT], BF16, name="phi_sb%d" % e) for e in range(EXPERTS)]
         x_sb = [keep.tile([P, TOKEN_TILES, FEAT], BF16, name="x_sb%d" % b) for b in range(BATCH)]
@@ -67,15 +67,15 @@ def tile_mixtureexpertsmlp_pb_e_kernel(tc, h, w2_words, w2_scales, b2, x, phi, o
             nc.sync.dma_start(out=phi_sb[e][:], in_=phi[e])
         for b in range(BATCH):
             nc.sync.dma_start(out=x_sb[b][:], in_=x[b].rearrange("(r m) d -> r m d", m=TOKEN_TILES))
-        for e in range(EXPERTS):
-            nc.sync.dma_start(out=h_sb[0][e][:], in_=h[0, e])
+        for b in range(BATCH):
+            for e in range(EXPERTS):
+                nc.sync.dma_start(out=h_sb[b][e][:], in_=h[b, e])
+                for quadrant in (2 * b, 2 * b + 1):
+                    nc.sync.dma_start(
+                        out=w_scales[32 * quadrant : 32 * quadrant + 16, e, :].bitcast(I32),
+                        in_=w2_scales[PASSES * e : PASSES * (e + 1), 4 * quadrant : 4 * quadrant + 4, :].bitcast(I32),
+                    )
         nc.sync.dma_start(out=b2_row[0:1, :], in_=b2.rearrange("(o e) d -> o (e d)", o=1))
-        for i in range(4):
-            nc.sync.dma_start(out=h_sb[1][i][:], in_=h[1, i])
-            nc.sync.dma_start(
-                out=w_scales[i : P : 32, :, :].bitcast(I32),
-                in_=w2_scales[:, i : 16 : 4, :].rearrange("g q n -> q g n").bitcast(I32),
-            )
         for e in range(EXPERTS):
             nc.sync.dma_start(
                 out=w_codes[e][:].bitcast(I32),
@@ -152,7 +152,7 @@ def tile_mixtureexpertsmlp_pb_e_kernel(tc, h, w2_words, w2_scales, b2, x, phi, o
                         lhsT=h_codes[b][e][:, g, :].bitcast(FP8X4),
                         lhsT_scale=h_scales[b][e][:, g, :],
                         rhs=w_codes[e][:, g, cols].bitcast(FP8X4),
-                        rhs_scale=w_scales[:, e * PASSES + g, cols],
+                        rhs_scale=w_scales[4 * g : P, e, cols],
                         start=(g == 0),
                         stop=(g == PASSES - 1),
                     )
@@ -192,9 +192,10 @@ def tile_mixtureexpertsmlp_pb_e_kernel(tc, h, w2_words, w2_scales, b2, x, phi, o
                         nc.vector.tensor_scalar_mul(
                             out=result[:, m, :], in0=combined[:, mm, :], scalar1=inv_sum[:, col : col + 1]
                         )
-            nc.sync.dma_start(
-                out=out[b].rearrange("(r m) d -> r m d", m=TOKEN_TILES)[:, :, j * P : (j + 1) * P], in_=result[:]
-            )
+                nc.sync.dma_start(
+                    out=out[b].rearrange("(r m) d -> r m d", m=TOKEN_TILES)[:, 2 * half : 2 * half + 2, j * P : (j + 1) * P],
+                    in_=result[:, 2 * half : 2 * half + 2, :],
+                )
 
         for e in range(EXPERTS):
             flipped = new_flipped_bf16()

@@ -36,8 +36,8 @@ def tile_mixtureexpertsmlp_pb_e_kernel(tc, h, w2_words, w2_scales, b2, x, phi, o
         ctx.enter_context(tc.manual_schedule())
         keep = ctx.enter_context(tc.tile_pool(name="keep", bufs=1))
         stage = ctx.enter_context(tc.tile_pool(name="stage", bufs=3))
-        psum_small = ctx.enter_context(tc.psum_pool(name="psum_small", bufs=5))
-        psum_wide = ctx.enter_context(tc.psum_pool(name="psum_wide", bufs=3))
+        psum_small = ctx.enter_context(tc.psum_pool(name="psum_small", bufs=6))
+        psum_wide = ctx.enter_context(tc.psum_pool(name="psum_wide", bufs=2))
 
         def copy_out(piece, out_ap, in_ap):
             if piece % 2 == 0:
@@ -63,10 +63,10 @@ def tile_mixtureexpertsmlp_pb_e_kernel(tc, h, w2_words, w2_scales, b2, x, phi, o
         x_sb = [keep.tile([P, TOKEN_TILES, FEAT], BF16, name="x_sb%d" % b) for b in range(BATCH)]
         h_sb = [[keep.tile([P, HIDDEN], BF16, name="h_sb%d_%d" % (b, e)) for e in range(EXPERTS)] for b in range(BATCH)]
         w_codes = [keep.tile([P, PASSES, FEAT], U32, name="w_codes%d" % e, align_bytes=64) for e in range(EXPERTS)]
+        x_tiled = [x[b].rearrange("(r m) d -> r m d", m=TOKEN_TILES) for b in range(BATCH)]
+        nc.sync.dma_start(out=x_sb[0][:, 0:2, :], in_=x_tiled[0][:, 0:2, :])
         for e in range(EXPERTS):
             nc.sync.dma_start(out=phi_sb[e][:], in_=phi[e])
-        for b in range(BATCH):
-            nc.sync.dma_start(out=x_sb[b][:], in_=x[b].rearrange("(r m) d -> r m d", m=TOKEN_TILES))
         for b in range(BATCH):
             for e in range(EXPERTS):
                 nc.sync.dma_start(out=h_sb[b][e][:], in_=h[b, e])
@@ -75,6 +75,10 @@ def tile_mixtureexpertsmlp_pb_e_kernel(tc, h, w2_words, w2_scales, b2, x, phi, o
                         out=w_scales[32 * quadrant : 32 * quadrant + 16, e, :].bitcast(I32),
                         in_=w2_scales[PASSES * e : PASSES * (e + 1), 4 * quadrant : 4 * quadrant + 4, :].bitcast(I32),
                     )
+                if (b, e) == (0, 0):
+                    nc.sync.dma_start(out=x_sb[0][:, 2:4, :], in_=x_tiled[0][:, 2:4, :])
+                if (b, e) == (0, 1):
+                    nc.sync.dma_start(out=x_sb[1][:], in_=x_tiled[1])
         nc.sync.dma_start(out=b2_row[0:1, :], in_=b2.rearrange("(o e) d -> o (e d)", o=1))
         for e in range(EXPERTS):
             nc.sync.dma_start(
@@ -197,56 +201,66 @@ def tile_mixtureexpertsmlp_pb_e_kernel(tc, h, w2_words, w2_scales, b2, x, phi, o
                     in_=result[:, 2 * half : 2 * half + 2, :],
                 )
 
+        flipped = new_flipped_bf16()
+        for c in range(FEAT_BLOCKS):
+            transpose_x(0, 0, c, flipped)
+        nc.vector.tensor_copy(out=xT[0][:, 0, :, :], in_=flipped[:])
         for e in range(EXPERTS):
             flipped = new_flipped_bf16()
             for c in range(FEAT_BLOCKS):
                 transpose_phi(e, c, flipped)
-            copy_out(e, phiT[:, :, e * P : (e + 1) * P], flipped[:])
-        for m in range(TOKEN_TILES):
-            flipped = new_flipped_bf16()
-            for c in range(FEAT_BLOCKS):
-                transpose_x(0, m, c, flipped)
-            copy_out(m, xT[0][:, m, :, :], flipped[:])
+            copy_out(e + 1, phiT[:, :, e * P : (e + 1) * P], flipped[:])
 
-        waiting_h = None
-        for b in range(BATCH):
-            for m in range(TOKEN_TILES):
-                col = b * TOKEN_TILES + m
-                logits = psum_wide.tile([P, ALL_SLOTS], F32, tag="wide", name="logits")
-                flipped = new_flipped_bf16()
-                flipped_words = [new_flipped_words(), new_flipped_words()]
-                for c in range(FEAT_BLOCKS):
-                    nc.tensor.matmul(
-                        out=logits[:], lhsT=xT[b][:, m, c, :], rhs=phiT[:, c, :],
-                        start=(c == 0), stop=(c == FEAT_BLOCKS - 1),
-                    )
-                    if b == 0:
-                        transpose_x(1, m, c, flipped)
-                    else:
-                        transpose_p(0, m, c, flipped)
-                    for u in range(2):
-                        transpose_h(b, m, c, u, flipped_words[c // 2])
-                nc.vector.tensor_reduce(
-                    out=neg_max[:, col : col + 1], in_=logits[:], axis=AXIS.X, op=ALU.max, negate=True
+        tiles = [(b, m) for b in range(BATCH) for m in range(TOKEN_TILES)]
+
+        def exponential(i):
+            b, m = tiles[i]
+            nc.scalar.activation(
+                out=p_bf[b][m][:], in_=all_logits[i][:], func=ACT.Exp,
+                bias=neg_max[:, i : i + 1], scale=1.0, accum_out=p_sum[:, i : i + 1],
+            )
+
+        all_logits = []
+        for i in range(len(tiles)):
+            b, m = tiles[i]
+            following = tiles[i + 1] if i + 1 < len(tiles) else None
+            earlier = tiles[i - 2] if i >= 2 else None
+            logits = psum_wide.tile([P, ALL_SLOTS], F32, tag="wide", name="logits")
+            all_logits.append(logits)
+            h_grouped = stage.tile([P, PASSES, P, PACK], BF16, name="h_grouped", align_bytes=64)
+            for c in range(FEAT_BLOCKS):
+                nc.tensor.matmul(
+                    out=logits[:], lhsT=xT[b][:, m, c, :], rhs=phiT[:, c, :],
+                    start=(c == 0), stop=(c == FEAT_BLOCKS - 1),
                 )
-                h_grouped = stage.tile([P, PASSES, P, PACK], BF16, name="h_grouped", align_bytes=64)
-                for half in range(2):
-                    regroup_h(half, h_grouped, flipped_words[half])
-                nc.scalar.activation(
-                    out=p_bf[b][m][:], in_=logits[:], func=ACT.Exp,
-                    bias=neg_max[:, col : col + 1], scale=1.0, accum_out=p_sum[:, col : col + 1],
-                )
-                if b == 0:
-                    nc.vector.tensor_copy(out=xT[1][:, m, :, :], in_=flipped[:])
-                else:
-                    regroup_p(0, 0, m, flipped)
-                    if m > 0:
-                        quantise_p(0, m - 1)
-                if waiting_h is not None:
-                    quantise_h(*waiting_h)
-                waiting_h = (b, m, h_grouped)
-        quantise_p(0, TOKEN_TILES - 1)
-        quantise_h(*waiting_h)
+                if c == 0 and following is not None:
+                    flipped_x = new_flipped_bf16()
+                if c == 2 and earlier is not None:
+                    flipped_p = new_flipped_bf16()
+                for piece in (2 * (c % 2), 2 * (c % 2) + 1):
+                    if c < 2 and following is not None:
+                        transpose_x(following[0], following[1], piece, flipped_x)
+                    if c >= 2 and earlier is not None:
+                        transpose_p(earlier[0], earlier[1], piece, flipped_p)
+                if c % 2 == 0:
+                    flipped_words = new_flipped_words()
+                for u in range(2):
+                    transpose_h(b, m, c, u, flipped_words)
+                if c == 0 and i >= 1:
+                    exponential(i - 1)
+                if c == 1 and following is not None:
+                    nc.scalar.copy(out=xT[following[0]][:, following[1], :, :], in_=flipped_x[:])
+                if c % 2 == 1:
+                    regroup_h(c // 2, h_grouped, flipped_words)
+            nc.vector.tensor_reduce(
+                out=neg_max[:, i : i + 1], in_=logits[:], axis=AXIS.X, op=ALU.max, negate=True
+            )
+            if earlier is not None:
+                regroup_p(0, earlier[0], earlier[1], flipped_p)
+            quantise_h(b, m, h_grouped)
+            if earlier is not None:
+                quantise_p(earlier[0], earlier[1])
+        exponential(len(tiles) - 1)
 
         for j in range(FEAT_BLOCKS):
             spread = psum_small.tile([P, EXPERTS, P], F32, tag="small", name="bias_spread")
@@ -255,15 +269,15 @@ def tile_mixtureexpertsmlp_pb_e_kernel(tc, h, w2_words, w2_scales, b2, x, phi, o
                 nc.tensor.matmul(
                     out=spread[:, e, :], lhsT=ones_bf[:], rhs=b2_row[:, first : first + P], start=True, stop=True
                 )
-            copy_out(j, bias_sb[:, j, :, :], spread[:].rearrange("s e d -> s d e"))
-        for m in range(TOKEN_TILES):
+            copy_out(0 if j == 0 else 1, bias_sb[:, j, :, :], spread[:].rearrange("s e d -> s d e"))
+        for piece in range(2):
+            b, m = tiles[len(tiles) - 2 + piece]
             flipped = new_flipped_bf16()
             for e in range(EXPERTS):
-                transpose_p(1, m, e, flipped)
-            regroup_p(m, 1, m, flipped)
-            if m > 0:
-                quantise_p(1, m - 1)
-        quantise_p(1, TOKEN_TILES - 1)
+                transpose_p(b, m, e, flipped)
+            regroup_p(piece, b, m, flipped)
+        for piece in range(2):
+            quantise_p(*tiles[len(tiles) - 2 + piece])
         nc.vector.reciprocal(out=inv_sum[:], in_=p_sum[:])
 
         blocks = [(b, j) for b in range(BATCH) for j in range(FEAT_BLOCKS)]

@@ -65,8 +65,10 @@ def tile_mixtureexpertsmlp_pb_e_kernel(tc, h, w2_words, w2_scales, b2, x, phi, o
         w_codes = [keep.tile([P, PASSES, FEAT], U32, name="w_codes%d" % e, align_bytes=64) for e in range(EXPERTS)]
         x_tiled = [x[b].rearrange("(r m) d -> r m d", m=TOKEN_TILES) for b in range(BATCH)]
         nc.sync.dma_start(out=x_sb[0][:, 0:2, :], in_=x_tiled[0][:, 0:2, :])
-        for e in range(EXPERTS):
-            nc.sync.dma_start(out=phi_sb[e][:], in_=phi[e])
+        for q in range(EXPERTS):
+            for v in range(2):
+                first = (SLOTS // 2) * (q % 2)
+                nc.sync.dma_start(out=phi_sb[q][v:P:2, :], in_=phi[2 * (q // 2) + v, first : first + SLOTS // 2, :])
         for b in range(BATCH):
             for e in range(EXPERTS):
                 nc.sync.dma_start(out=h_sb[b][e][:], in_=h[b, e])
@@ -110,11 +112,14 @@ def tile_mixtureexpertsmlp_pb_e_kernel(tc, h, w2_words, w2_scales, b2, x, phi, o
         def transpose_x(b, m, c, flipped):
             nc.tensor.transpose(flipped[:, c, :], x_sb[b][:, m, c * P : (c + 1) * P], ident_bf[:])
 
-        def transpose_p(b, m, e, flipped):
-            nc.tensor.transpose(flipped[:, e, :], p_bf[b][m][:, e * P : (e + 1) * P], ident_bf[:])
+        def new_flipped_p():
+            return psum_small.tile([P, 2, P], F32, tag="small", name="flipped_p")
+
+        def transpose_p(b, m, pair, flipped):
+            nc.tensor.transpose(flipped[:, pair, :], p_bf[b][m][:].bitcast(F32)[:, pair * P : (pair + 1) * P], ident_f32[:])
 
         def regroup_p(piece, b, m, flipped):
-            copy_out(piece, p_grouped[b][:, m, :, :], flipped[:].rearrange("s e r -> s r e"))
+            copy_out(piece, p_grouped[b][:, m, :, :].bitcast(F32), flipped[:].rearrange("s pair r -> s r pair"))
 
         def quantise_p(b, m):
             nc.vector.quantize_mx(
@@ -236,12 +241,12 @@ def tile_mixtureexpertsmlp_pb_e_kernel(tc, h, w2_words, w2_scales, b2, x, phi, o
                 if c == 0 and following is not None:
                     flipped_x = new_flipped_bf16()
                 if c == 2 and earlier is not None:
-                    flipped_p = new_flipped_bf16()
-                for piece in (2 * (c % 2), 2 * (c % 2) + 1):
-                    if c < 2 and following is not None:
+                    flipped_p = new_flipped_p()
+                if c < 2 and following is not None:
+                    for piece in (2 * c, 2 * c + 1):
                         transpose_x(following[0], following[1], piece, flipped_x)
-                    if c >= 2 and earlier is not None:
-                        transpose_p(earlier[0], earlier[1], piece, flipped_p)
+                if c >= 2 and earlier is not None:
+                    transpose_p(earlier[0], earlier[1], c - 2, flipped_p)
                 if c % 2 == 0:
                     flipped_words = new_flipped_words()
                 for u in range(2):
@@ -272,9 +277,9 @@ def tile_mixtureexpertsmlp_pb_e_kernel(tc, h, w2_words, w2_scales, b2, x, phi, o
             copy_out(0 if j == 0 else 1, bias_sb[:, j, :, :], spread[:].rearrange("s e d -> s d e"))
         for piece in range(2):
             b, m = tiles[len(tiles) - 2 + piece]
-            flipped = new_flipped_bf16()
-            for e in range(EXPERTS):
-                transpose_p(b, m, e, flipped)
+            flipped = new_flipped_p()
+            for pair in range(2):
+                transpose_p(b, m, pair, flipped)
             regroup_p(piece, b, m, flipped)
         for piece in range(2):
             quantise_p(*tiles[len(tiles) - 2 + piece])

@@ -253,8 +253,11 @@ def tile_mixtureexpertsmlp_pb_e_kernel(tc, h, w2_words, w2_scales, b2, x, phi, o
                     transpose_h(b, m, c, u, flipped_words)
                 if c == 0 and i >= 1:
                     exponential(i - 1)
-                if c == 1 and following is not None:
-                    nc.scalar.copy(out=xT[following[0]][:, following[1], :, :], in_=flipped_x[:])
+                if c == 1:
+                    if following is not None:
+                        nc.vector.tensor_copy(out=xT[following[0]][:, following[1], :, :], in_=flipped_x[:])
+                    if i >= 3:
+                        quantise_p(*tiles[i - 3])
                 if c % 2 == 1:
                     regroup_h(c // 2, h_grouped, flipped_words)
             nc.vector.tensor_reduce(
@@ -263,9 +266,8 @@ def tile_mixtureexpertsmlp_pb_e_kernel(tc, h, w2_words, w2_scales, b2, x, phi, o
             if earlier is not None:
                 regroup_p(0, earlier[0], earlier[1], flipped_p)
             quantise_h(b, m, h_grouped)
-            if earlier is not None:
-                quantise_p(earlier[0], earlier[1])
         exponential(len(tiles) - 1)
+        quantise_p(*tiles[len(tiles) - 3])
 
         for j in range(FEAT_BLOCKS):
             spread = psum_small.tile([P, EXPERTS, P], F32, tag="small", name="bias_spread")

@@ -36,6 +36,7 @@ def tile_mixtureexpertsmlp_pb_e_kernel(tc, h, w2_words, w2_scales, b2, x, phi, o
         ctx.enter_context(tc.manual_schedule())
         keep = ctx.enter_context(tc.tile_pool(name="keep", bufs=1))
         stage = ctx.enter_context(tc.tile_pool(name="stage", bufs=3))
+        results = ctx.enter_context(tc.tile_pool(name="results", bufs=BATCH * FEAT_BLOCKS))
         psum_small = ctx.enter_context(tc.psum_pool(name="psum_small", bufs=6))
         psum_wide = ctx.enter_context(tc.psum_pool(name="psum_wide", bufs=2))
 
@@ -151,10 +152,12 @@ def tile_mixtureexpertsmlp_pb_e_kernel(tc, h, w2_words, w2_scales, b2, x, phi, o
                 in_=grouped[:].rearrange("r g s t -> r (g s t)"),
             )
 
-        def first_layer(b, j):
+        def new_y_bank():
+            return psum_small.tile([P, EXPERTS, P], F32, tag="small", name="y_psum")
+
+        def first_layer_passes(b, j, experts, y_psum):
             cols = slice(j * P, (j + 1) * P)
-            y_psum = psum_small.tile([P, EXPERTS, P], F32, tag="small", name="y_psum")
-            for e in range(EXPERTS):
+            for e in experts:
                 for g in range(PASSES):
                     nc.tensor.matmul_mx(
                         out=y_psum[:, e, :],
@@ -165,6 +168,8 @@ def tile_mixtureexpertsmlp_pb_e_kernel(tc, h, w2_words, w2_scales, b2, x, phi, o
                         start=(g == 0),
                         stop=(g == PASSES - 1),
                     )
+
+        def pack_y(b, j, y_psum):
             y_grouped = stage.tile([P, P, PACK], BF16, name="y_grouped", align_bytes=64)
             nc.vector.tensor_tensor(
                 out=y_grouped[:], in0=y_psum[:].rearrange("s e d -> s d e"), in1=bias_sb[:, j, :, :], op=ALU.add
@@ -176,9 +181,12 @@ def tile_mixtureexpertsmlp_pb_e_kernel(tc, h, w2_words, w2_scales, b2, x, phi, o
             )
 
         def combine(b, j, vector_helps):
-            result = stage.tile([P, TOKEN_TILES, P], F32, name="result")
+            result = results.tile([P, TOKEN_TILES, P], F32, name="result")
             for half in range(2):
-                combined = psum_wide.tile([P, 2, P], F32, tag="wide", name="combined")
+                if half == 0:
+                    combined = psum_wide.tile([P, 2, P], F32, tag="wide", name="combined")
+                else:
+                    combined = psum_small.tile([P, 2, P], F32, tag="small", name="combined")
                 for mm in range(2):
                     m = 2 * half + mm
                     nc.tensor.matmul_mx(
@@ -288,9 +296,16 @@ def tile_mixtureexpertsmlp_pb_e_kernel(tc, h, w2_words, w2_scales, b2, x, phi, o
         nc.vector.reciprocal(out=inv_sum[:], in_=p_sum[:])
 
         blocks = [(b, j) for b in range(BATCH) for j in range(FEAT_BLOCKS)]
-        for i in range(len(blocks) + COMBINE_LAG):
+        first_banks = [new_y_bank() for i in range(COMBINE_LAG)]
+        for i in range(COMBINE_LAG):
+            first_layer_passes(blocks[i][0], blocks[i][1], range(EXPERTS - 1), first_banks[i])
+        for i in range(COMBINE_LAG):
+            first_layer_passes(blocks[i][0], blocks[i][1], range(EXPERTS - 1, EXPERTS), first_banks[i])
+            pack_y(blocks[i][0], blocks[i][1], first_banks[i])
+        for i in range(COMBINE_LAG, len(blocks) + COMBINE_LAG):
             if i < len(blocks):
-                first_layer(*blocks[i])
-            if i >= COMBINE_LAG:
-                b, j = blocks[i - COMBINE_LAG]
-                combine(b, j, i >= len(blocks))
+                y_psum = new_y_bank()
+                first_layer_passes(blocks[i][0], blocks[i][1], range(EXPERTS), y_psum)
+                pack_y(blocks[i][0], blocks[i][1], y_psum)
+            b, j = blocks[i - COMBINE_LAG]
+            combine(b, j, i >= len(blocks))

@@ -46,10 +46,12 @@ def tile_mixtureexpertsmlp_pb_e_kernel(tc, h, w2_words, w2_scales, b2, x, phi, o
             else:
                 nc.scalar.copy(out=out_ap, in_=in_ap)
 
-        b2_row = keep.tile([P, EXPERTS * FEAT], BF16, name="b2_row")
-        nc.vector.memset(b2_row[:].bitcast(I32), 0)
         ones_bf = keep.tile([P, P], BF16, name="ones_bf")
         nc.vector.memset(ones_bf[:], 1.0)
+        idle_rhs = keep.tile([P, ALL_SLOTS], BF16, name="idle_rhs")
+        nc.vector.memset(idle_rhs[:], 0.0)
+        b2_row = keep.tile([P, EXPERTS * FEAT], BF16, name="b2_row")
+        nc.vector.memset(b2_row[:].bitcast(I32), 0)
         warm = keep.tile([P, 1], F32, name="warm")
         nc.vector.memset(warm[:], 0.0)
         nc.scalar.activation(out=warm[:], in_=warm[:], func=ACT.Exp)
@@ -214,6 +216,12 @@ def tile_mixtureexpertsmlp_pb_e_kernel(tc, h, w2_words, w2_scales, b2, x, phi, o
                     in_=result[:, 2 * half : 2 * half + 2, :],
                 )
 
+        def keep_busy(count):
+            unread = psum_wide.tile([P, ALL_SLOTS], F32, tag="wide", name="unread")
+            for k in range(count):
+                nc.tensor.matmul(out=unread[:], lhsT=ones_bf[:], rhs=idle_rhs[:], start=True, stop=True)
+
+        keep_busy(4)
         flipped = new_flipped_bf16()
         for c in range(FEAT_BLOCKS):
             transpose_x(0, 0, c, flipped)
@@ -223,6 +231,8 @@ def tile_mixtureexpertsmlp_pb_e_kernel(tc, h, w2_words, w2_scales, b2, x, phi, o
             for c in range(FEAT_BLOCKS):
                 transpose_phi(e, c, flipped)
             copy_out(e + 1, phiT[:, :, e * P : (e + 1) * P], flipped[:])
+            if e % 2 == 1:
+                keep_busy(1)
 
         tiles = [(b, m) for b in range(BATCH) for m in range(TOKEN_TILES)]
 

@@ -306,7 +306,7 @@ def tile_mixtureexpertsmlp_pb_e_kernel(tc, h, w2_words, w2_scales, b2, x, phi, o
         nc.vector.reciprocal(out=inv_sum[:], in_=p_sum[:])
 
         blocks = [(b, j) for b in range(BATCH) for j in range(FEAT_BLOCKS)]
-        first_banks = [new_y_bank() for i in range(COMBINE_LAG)]
+        first_banks = [psum_wide.tile([P, EXPERTS, P], F32, tag="wide", name="y_psum_first") for i in range(COMBINE_LAG)]
         for i in range(COMBINE_LAG):
             first_layer_passes(blocks[i][0], blocks[i][1], range(EXPERTS - 1), first_banks[i])
         for i in range(COMBINE_LAG):

@@ -65,7 +65,7 @@ def tile_mixtureexpertsmlp_pb_e_kernel(tc, h, w2_words, w2_scales, b2, x, phi, o
         phi_sb = [keep.tile([P, FEAT], BF16, name="phi_sb%d" % e) for e in range(EXPERTS)]
         x_sb = [keep.tile([P, TOKEN_TILES, FEAT], BF16, name="x_sb%d" % b) for b in range(BATCH)]
         h_sb = [[keep.tile([P, HIDDEN], BF16, name="h_sb%d_%d" % (b, e)) for e in range(EXPERTS)] for b in range(BATCH)]
-        w_codes = [keep.tile([P, PASSES, FEAT], U32, name="w_codes%d" % e, align_bytes=64) for e in range(EXPERTS)]
+        w_codes = keep.tile([P, EXPERTS * PASSES, FEAT], U32, name="w_codes", align_bytes=64)
         x_tiled = [x[b].rearrange("(r m) d -> r m d", m=TOKEN_TILES) for b in range(BATCH)]
         nc.sync.dma_start(out=x_sb[0][:, 0:2, :], in_=x_tiled[0][:, 0:2, :])
         for q in range(EXPERTS):
@@ -85,11 +85,14 @@ def tile_mixtureexpertsmlp_pb_e_kernel(tc, h, w2_words, w2_scales, b2, x, phi, o
                 if (b, e) == (0, 1):
                     nc.sync.dma_start(out=x_sb[1][:], in_=x_tiled[1])
         nc.sync.dma_start(out=b2_row[0:1, :], in_=b2.rearrange("(o e) d -> o (e d)", o=1))
-        for e in range(EXPERTS):
-            nc.sync.dma_start(
-                out=w_codes[e][:].bitcast(I32),
-                in_=w2_words[PASSES * e : PASSES * (e + 1)].rearrange("g r n t -> r g (n t)").bitcast(I32),
-            )
+        for half in range(2):
+            cols = slice(half * (FEAT // 2), (half + 1) * (FEAT // 2))
+            for k in range(EXPERTS // 2):
+                groups = slice(2 * k * PASSES, 2 * (k + 1) * PASSES)
+                nc.sync.dma_start(
+                    out=w_codes[:, groups, cols].bitcast(I32),
+                    in_=w2_words[groups, :, cols, :].rearrange("g r n t -> r g (n t)").bitcast(I32),
+                )
 
         phiT = keep.tile([P, FEAT_BLOCKS, ALL_SLOTS], BF16, name="phiT")
         xT = [keep.tile([P, TOKEN_TILES, FEAT_BLOCKS, P], BF16, name="xT%d" % b) for b in range(BATCH)]
@@ -165,7 +168,7 @@ def tile_mixtureexpertsmlp_pb_e_kernel(tc, h, w2_words, w2_scales, b2, x, phi, o
                         out=y_psum[:, e, :],
                         lhsT=h_codes[b][e][:, g, :].bitcast(FP8X4),
                         lhsT_scale=h_scales[b][e][:, g, :],
-                        rhs=w_codes[e][:, g, cols].bitcast(FP8X4),
+                        rhs=w_codes[:, PASSES * e + g, cols].bitcast(FP8X4),
                         rhs_scale=w_scales[4 * g : P, e, cols],
                         start=(g == 0),
                         stop=(g == PASSES - 1),
@@ -305,17 +308,15 @@ def tile_mixtureexpertsmlp_pb_e_kernel(tc, h, w2_words, w2_scales, b2, x, phi, o
             quantise_p(*tiles[len(tiles) - 2 + piece])
         nc.vector.reciprocal(out=inv_sum[:], in_=p_sum[:])
 
-        blocks = [(b, j) for b in range(BATCH) for j in range(FEAT_BLOCKS)]
-        first_banks = [psum_wide.tile([P, EXPERTS, P], F32, tag="wide", name="y_psum_first") for i in range(COMBINE_LAG)]
-        for i in range(COMBINE_LAG):
-            first_layer_passes(blocks[i][0], blocks[i][1], range(EXPERTS - 1), first_banks[i])
-        for i in range(COMBINE_LAG):
-            first_layer_passes(blocks[i][0], blocks[i][1], range(EXPERTS - 1, EXPERTS), first_banks[i])
-            pack_y(blocks[i][0], blocks[i][1], first_banks[i])
-        for i in range(COMBINE_LAG, len(blocks) + COMBINE_LAG):
+        blocks = [(b, 2 * half + jj) for half in range(2) for b in range(BATCH) for jj in range(2)]
+        for i in range(len(blocks) + COMBINE_LAG):
             if i < len(blocks):
-                y_psum = new_y_bank()
+                if i < COMBINE_LAG:
+                    y_psum = psum_wide.tile([P, EXPERTS, P], F32, tag="wide", name="y_psum_first")
+                else:
+                    y_psum = new_y_bank()
                 first_layer_passes(blocks[i][0], blocks[i][1], range(EXPERTS), y_psum)
                 pack_y(blocks[i][0], blocks[i][1], y_psum)
-            b, j = blocks[i - COMBINE_LAG]
-            combine(b, j, i >= len(blocks))
+            if i >= COMBINE_LAG:
+                b, j = blocks[i - COMBINE_LAG]
+                combine(b, j, i >= len(blocks))

@@ -55,9 +55,7 @@ def tile_mixtureexpertsmlp_pb_e_kernel(tc, h, w2_words, w2_scales, b2, x, phi, o
         warm = keep.tile([P, 1], F32, name="warm")
         nc.vector.memset(warm[:], 0.0)
         nc.scalar.activation(out=warm[:], in_=warm[:], func=ACT.Exp)
-        ident_bf = keep.tile([P, P], BF16, name="ident_bf")
         ident_f32 = keep.tile([P, P], F32, name="ident_f32")
-        make_identity(nc, ident_bf[:])
         make_identity(nc, ident_f32[:])
         w_scales = keep.tile([P, EXPERTS, FEAT], U8, name="w_scales", align_bytes=64)
         nc.vector.memset(w_scales[:].rearrange("r e n -> r (e n)").bitcast(I32), 0)
@@ -95,7 +93,7 @@ def tile_mixtureexpertsmlp_pb_e_kernel(tc, h, w2_words, w2_scales, b2, x, phi, o
                 )
 
         phiT = keep.tile([P, FEAT_BLOCKS, ALL_SLOTS], BF16, name="phiT")
-        xT = [keep.tile([P, TOKEN_TILES, FEAT_BLOCKS, P], BF16, name="xT%d" % b) for b in range(BATCH)]
+        xT = [keep.tile([P, TOKEN_TILES, 2, P, 2], BF16, name="xT%d" % b) for b in range(BATCH)]
         p_bf = [[keep.tile([P, ALL_SLOTS], BF16, name="p_bf%d_%d" % (b, m)) for m in range(TOKEN_TILES)] for b in range(BATCH)]
         neg_max = keep.tile([P, BATCH * TOKEN_TILES], F32, name="neg_max")
         p_sum = keep.tile([P, BATCH * TOKEN_TILES], F32, name="p_sum")
@@ -109,17 +107,19 @@ def tile_mixtureexpertsmlp_pb_e_kernel(tc, h, w2_words, w2_scales, b2, x, phi, o
         y_codes = [[keep.tile([P, P], U32, name="y_codes%d_%d" % (b, j), align_bytes=64) for j in range(FEAT_BLOCKS)] for b in range(BATCH)]
         y_scales = [[keep.tile([P, P], U8, name="y_scales%d_%d" % (b, j), align_bytes=64) for j in range(FEAT_BLOCKS)] for b in range(BATCH)]
 
-        def new_flipped_bf16():
-            return psum_small.tile([P, 4, P], BF16, tag="small", name="flipped_bf16")
+        def new_flipped():
+            return psum_small.tile([P, 2, P], F32, tag="small", name="flipped")
 
-        def transpose_phi(e, c, flipped):
-            nc.tensor.transpose(flipped[:, c, :], phi_sb[e][:, c * P : (c + 1) * P], ident_bf[:])
+        def transpose_phi(q, u, flipped):
+            nc.tensor.transpose(flipped[:, u, :], phi_sb[q][:].bitcast(F32)[:, u * P : (u + 1) * P], ident_f32[:])
 
-        def transpose_x(b, m, c, flipped):
-            nc.tensor.transpose(flipped[:, c, :], x_sb[b][:, m, c * P : (c + 1) * P], ident_bf[:])
+        def transpose_x(b, m, u, flipped):
+            nc.tensor.transpose(flipped[:, u, :], x_sb[b][:, m, :].bitcast(F32)[:, u * P : (u + 1) * P], ident_f32[:])
 
-        def new_flipped_p():
-            return psum_small.tile([P, 2, P], F32, tag="small", name="flipped_p")
+        def keep_x(b, m, flipped):
+            nc.vector.tensor_copy(
+                out=xT[b][:, m, :, :, :].rearrange("d u r v -> d (u r v)").bitcast(F32), in_=flipped[:].rearrange("d u r -> d (u r)")
+            )
 
         def transpose_p(b, m, pair, flipped):
             nc.tensor.transpose(flipped[:, pair, :], p_bf[b][m][:].bitcast(F32)[:, pair * P : (pair + 1) * P], ident_f32[:])
@@ -225,16 +225,20 @@ def tile_mixtureexpertsmlp_pb_e_kernel(tc, h, w2_words, w2_scales, b2, x, phi, o
                 nc.tensor.matmul(out=unread[:], lhsT=ones_bf[:], rhs=idle_rhs[:], start=True, stop=True)
 
         keep_busy(4)
-        flipped = new_flipped_bf16()
-        for c in range(FEAT_BLOCKS):
-            transpose_x(0, 0, c, flipped)
-        nc.vector.tensor_copy(out=xT[0][:, 0, :, :], in_=flipped[:])
-        for e in range(EXPERTS):
-            flipped = new_flipped_bf16()
-            for c in range(FEAT_BLOCKS):
-                transpose_phi(e, c, flipped)
-            copy_out(e + 1, phiT[:, :, e * P : (e + 1) * P], flipped[:])
-            if e % 2 == 1:
+        flipped = new_flipped()
+        for u in range(2):
+            transpose_x(0, 0, u, flipped)
+        keep_x(0, 0, flipped)
+        for q in range(EXPERTS):
+            for u in range(2):
+                flipped = new_flipped()
+                transpose_phi(q, u, flipped)
+                copy_out(
+                    u,
+                    phiT[:, 2 * u : 2 * u + 2, q * P : (q + 1) * P],
+                    flipped[:, u, :].bitcast(BF16).rearrange("d (s v) -> d v s", v=2),
+                )
+            if q % 2 == 1:
                 keep_busy(1)
 
         tiles = [(b, m) for b in range(BATCH) for m in range(TOKEN_TILES)]
@@ -256,16 +260,15 @@ def tile_mixtureexpertsmlp_pb_e_kernel(tc, h, w2_words, w2_scales, b2, x, phi, o
             h_grouped = stage.tile([P, PASSES, P, PACK], BF16, name="h_grouped", align_bytes=64)
             for c in range(FEAT_BLOCKS):
                 nc.tensor.matmul(
-                    out=logits[:], lhsT=xT[b][:, m, c, :], rhs=phiT[:, c, :],
+                    out=logits[:], lhsT=xT[b][:, m, c // 2, :, c % 2], rhs=phiT[:, c, :],
                     start=(c == 0), stop=(c == FEAT_BLOCKS - 1),
                 )
                 if c == 0 and following is not None:
-                    flipped_x = new_flipped_bf16()
+                    flipped_x = new_flipped()
                 if c == 2 and earlier is not None:
-                    flipped_p = new_flipped_p()
+                    flipped_p = new_flipped()
                 if c < 2 and following is not None:
-                    for piece in (2 * c, 2 * c + 1):
-                        transpose_x(following[0], following[1], piece, flipped_x)
+                    transpose_x(following[0], following[1], c, flipped_x)
                 if c >= 2 and earlier is not None:
                     transpose_p(earlier[0], earlier[1], c - 2, flipped_p)
                 if c % 2 == 0:
@@ -276,7 +279,7 @@ def tile_mixtureexpertsmlp_pb_e_kernel(tc, h, w2_words, w2_scales, b2, x, phi, o
                     exponential(i - 1)
                 if c == 1:
                     if following is not None:
-                        nc.vector.tensor_copy(out=xT[following[0]][:, following[1], :, :], in_=flipped_x[:])
+                        keep_x(following[0], following[1], flipped_x)
                     if i >= 3:
                         quantise_p(*tiles[i - 3])
                 if c % 2 == 1:
@@ -300,7 +303,7 @@ def tile_mixtureexpertsmlp_pb_e_kernel(tc, h, w2_words, w2_scales, b2, x, phi, o
             copy_out(0 if j == 0 else 1, bias_sb[:, j, :, :], spread[:].rearrange("s e d -> s d e"))
         for piece in range(2):
             b, m = tiles[len(tiles) - 2 + piece]
-            flipped = new_flipped_p()
+            flipped = new_flipped()
             for pair in range(2):
                 transpose_p(b, m, pair, flipped)
             regroup_p(piece, b, m, flipped)

@@ -46,33 +46,40 @@ def tile_mixtureexpertsmlp_pb_e_kernel(tc, h, w2_words, w2_scales, b2, x, phi, o
             else:
                 nc.scalar.copy(out=out_ap, in_=in_ap)
 
-        ones_bf = keep.tile([P, P], BF16, name="ones_bf")
-        nc.vector.memset(ones_bf[:], 1.0)
+        b2_rows = keep.tile([P, P], BF16, name="b2_rows")
+        nc.vector.memset(b2_rows[:].bitcast(I32), 0)
         idle_rhs = keep.tile([P, ALL_SLOTS], BF16, name="idle_rhs")
-        nc.vector.memset(idle_rhs[:], 0.0)
-        b2_row = keep.tile([P, EXPERTS * FEAT], BF16, name="b2_row")
-        nc.vector.memset(b2_row[:].bitcast(I32), 0)
+        nc.vector.memset(idle_rhs[:].bitcast(I32), 0)
         warm = keep.tile([P, 1], F32, name="warm")
         nc.vector.memset(warm[:], 0.0)
         nc.scalar.activation(out=warm[:], in_=warm[:], func=ACT.Exp)
         ident_f32 = keep.tile([P, P], F32, name="ident_f32")
+        ident_bf = keep.tile([P, P], BF16, name="ident_bf")
+        make_identity(nc, ident_bf[:])
         make_identity(nc, ident_f32[:])
         w_scales = keep.tile([P, EXPERTS, FEAT], U8, name="w_scales", align_bytes=64)
         nc.vector.memset(w_scales[:].rearrange("r e n -> r (e n)").bitcast(I32), 0)
 
-        phi_sb = [keep.tile([P, FEAT], BF16, name="phi_sb%d" % e) for e in range(EXPERTS)]
+        phi_sb = keep.tile([P, EXPERTS, FEAT], BF16, name="phi_sb")
         x_sb = [keep.tile([P, TOKEN_TILES, FEAT], BF16, name="x_sb%d" % b) for b in range(BATCH)]
         h_sb = [[keep.tile([P, HIDDEN], BF16, name="h_sb%d_%d" % (b, e)) for e in range(EXPERTS)] for b in range(BATCH)]
         w_codes = keep.tile([P, EXPERTS * PASSES, FEAT], U32, name="w_codes", align_bytes=64)
         x_tiled = [x[b].rearrange("(r m) d -> r m d", m=TOKEN_TILES) for b in range(BATCH)]
-        nc.sync.dma_start(out=x_sb[0][:, 0:2, :], in_=x_tiled[0][:, 0:2, :])
-        for q in range(EXPERTS):
-            for v in range(2):
-                first = (SLOTS // 2) * (q % 2)
-                nc.sync.dma_start(out=phi_sb[q][v:P:2, :], in_=phi[2 * (q // 2) + v, first : first + SLOTS // 2, :])
+        nc.sync.dma_start(out=b2_rows[0 : EXPERTS * FEAT_BLOCKS, :], in_=b2.rearrange("e (j d) -> (e j) d", d=P))
+        nc.sync.dma_start(out=x_sb[0][:, 0:1, :], in_=x_tiled[0][:, 0:1, :])
+        for e in range(EXPERTS):
+            k, v = divmod(e, 2)
+            nc.sync.dma_start(
+                out=phi_sb[v:P:2, 2 * k : 2 * k + 2, :], in_=phi[e].rearrange("(s2 i) d -> i s2 d", s2=2)
+            )
+        for half in range(2):
+            cols = slice(half * (HIDDEN // 2), (half + 1) * (HIDDEN // 2))
+            nc.sync.dma_start(out=h_sb[0][0][:, cols], in_=h[0, 0, :, cols])
+        nc.sync.dma_start(out=x_sb[0][:, 1:2, :], in_=x_tiled[0][:, 1:2, :])
         for b in range(BATCH):
             for e in range(EXPERTS):
-                nc.sync.dma_start(out=h_sb[b][e][:], in_=h[b, e])
+                if (b, e) != (0, 0):
+                    nc.sync.dma_start(out=h_sb[b][e][:], in_=h[b, e])
                 for quadrant in (2 * b, 2 * b + 1):
                     nc.sync.dma_start(
                         out=w_scales[32 * quadrant : 32 * quadrant + 16, e, :].bitcast(I32),
@@ -82,7 +89,6 @@ def tile_mixtureexpertsmlp_pb_e_kernel(tc, h, w2_words, w2_scales, b2, x, phi, o
                     nc.sync.dma_start(out=x_sb[0][:, 2:4, :], in_=x_tiled[0][:, 2:4, :])
                 if (b, e) == (0, 1):
                     nc.sync.dma_start(out=x_sb[1][:], in_=x_tiled[1])
-        nc.sync.dma_start(out=b2_row[0:1, :], in_=b2.rearrange("(o e) d -> o (e d)", o=1))
         for half in range(2):
             cols = slice(half * (FEAT // 2), (half + 1) * (FEAT // 2))
             for k in range(EXPERTS // 2):
@@ -111,7 +117,7 @@ def tile_mixtureexpertsmlp_pb_e_kernel(tc, h, w2_words, w2_scales, b2, x, phi, o
             return psum_small.tile([P, 2, P], F32, tag="small", name="flipped")
 
         def transpose_phi(q, u, flipped):
-            nc.tensor.transpose(flipped[:, u, :], phi_sb[q][:].bitcast(F32)[:, u * P : (u + 1) * P], ident_f32[:])
+            nc.tensor.transpose(flipped[:, u, :], phi_sb[:, q, :].bitcast(F32)[:, u * P : (u + 1) * P], ident_f32[:])
 
         def transpose_x(b, m, u, flipped):
             nc.tensor.transpose(flipped[:, u, :], x_sb[b][:, m, :].bitcast(F32)[:, u * P : (u + 1) * P], ident_f32[:])
@@ -222,14 +228,26 @@ def tile_mixtureexpertsmlp_pb_e_kernel(tc, h, w2_words, w2_scales, b2, x, phi, o
         def keep_busy(count):
             unread = psum_wide.tile([P, ALL_SLOTS], F32, tag="wide", name="unread")
             for k in range(count):
-                nc.tensor.matmul(out=unread[:], lhsT=ones_bf[:], rhs=idle_rhs[:], start=True, stop=True)
+                nc.tensor.matmul(out=unread[:], lhsT=idle_rhs[:, 0:P], rhs=idle_rhs[:], start=True, stop=True)
 
-        keep_busy(4)
-        flipped = new_flipped()
-        for u in range(2):
-            transpose_x(0, 0, u, flipped)
-        keep_x(0, 0, flipped)
-        for q in range(EXPERTS):
+        def spread_bias(j, spread):
+            for e in range(EXPERTS):
+                row = e * FEAT_BLOCKS + j
+                nc.tensor.matmul(
+                    out=spread[:, e, :], lhsT=ident_bf[:, row : row + 1].to_broadcast([P, P]), rhs=b2_rows[:], start=True, stop=True
+                )
+            return spread
+
+        def keep_bias(piece, j, spread):
+            copy_out(piece, bias_sb[:, j, :, :], spread[:].rearrange("s e d -> s d e"))
+
+        def wide_bank():
+            return psum_wide.tile([P, EXPERTS, P], F32, tag="wide", name="bias_wide")
+
+        def small_bank():
+            return psum_small.tile([P, EXPERTS, P], F32, tag="small", name="bias_small")
+
+        def phi_tile(q):
             for u in range(2):
                 flipped = new_flipped()
                 transpose_phi(q, u, flipped)
@@ -238,8 +256,23 @@ def tile_mixtureexpertsmlp_pb_e_kernel(tc, h, w2_words, w2_scales, b2, x, phi, o
                     phiT[:, 2 * u : 2 * u + 2, q * P : (q + 1) * P],
                     flipped[:, u, :].bitcast(BF16).rearrange("d (s v) -> d v s", v=2),
                 )
-            if q % 2 == 1:
-                keep_busy(1)
+
+        keep_busy(4)
+        spreads = [spread_bias(j, wide_bank()) for j in range(2)]
+        flipped = new_flipped()
+        for u in range(2):
+            transpose_x(0, 0, u, flipped)
+        keep_x(0, 0, flipped)
+        keep_bias(1, 0, spreads[0])
+        phi_tile(0)
+        phi_tile(1)
+        spreads.append(spread_bias(2, small_bank()))
+        phi_tile(2)
+        phi_tile(3)
+        spreads.append(spread_bias(3, small_bank()))
+        keep_bias(0, 1, spreads[1])
+        keep_bias(1, 2, spreads[2])
+        keep_bias(0, 3, spreads[3])
 
         tiles = [(b, m) for b in range(BATCH) for m in range(TOKEN_TILES)]
 
@@ -258,17 +291,18 @@ def tile_mixtureexpertsmlp_pb_e_kernel(tc, h, w2_words, w2_scales, b2, x, phi, o
             logits = psum_wide.tile([P, ALL_SLOTS], F32, tag="wide", name="logits")
             all_logits.append(logits)
             h_grouped = stage.tile([P, PASSES, P, PACK], BF16, name="h_grouped", align_bytes=64)
+            x_round = 1 if i == 0 else 0
             for c in range(FEAT_BLOCKS):
                 nc.tensor.matmul(
                     out=logits[:], lhsT=xT[b][:, m, c // 2, :, c % 2], rhs=phiT[:, c, :],
                     start=(c == 0), stop=(c == FEAT_BLOCKS - 1),
                 )
-                if c == 0 and following is not None:
+                if c == x_round and following is not None:
                     flipped_x = new_flipped()
                 if c == 2 and earlier is not None:
                     flipped_p = new_flipped()
-                if c < 2 and following is not None:
-                    transpose_x(following[0], following[1], c, flipped_x)
+                if c in (x_round, x_round + 1) and following is not None:
+                    transpose_x(following[0], following[1], c - x_round, flipped_x)
                 if c >= 2 and earlier is not None:
                     transpose_p(earlier[0], earlier[1], c - 2, flipped_p)
                 if c % 2 == 0:
@@ -277,11 +311,10 @@ def tile_mixtureexpertsmlp_pb_e_kernel(tc, h, w2_words, w2_scales, b2, x, phi, o
                     transpose_h(b, m, c, u, flipped_words)
                 if c == 0 and i >= 1:
                     exponential(i - 1)
-                if c == 1:
-                    if following is not None:
-                        keep_x(following[0], following[1], flipped_x)
-                    if i >= 3:
-                        quantise_p(*tiles[i - 3])
+                if c == x_round + 1 and following is not None:
+                    keep_x(following[0], following[1], flipped_x)
+                if c == 1 and i >= 3:
+                    quantise_p(*tiles[i - 3])
                 if c % 2 == 1:
                     regroup_h(c // 2, h_grouped, flipped_words)
             nc.vector.tensor_reduce(
@@ -289,27 +322,20 @@ def tile_mixtureexpertsmlp_pb_e_kernel(tc, h, w2_words, w2_scales, b2, x, phi, o
             )
             if earlier is not None:
                 regroup_p(0, earlier[0], earlier[1], flipped_p)
-            quantise_h(b, m, h_grouped)
-        exponential(len(tiles) - 1)
-        quantise_p(*tiles[len(tiles) - 3])
-
-        for j in range(FEAT_BLOCKS):
-            spread = psum_small.tile([P, EXPERTS, P], F32, tag="small", name="bias_spread")
-            for e in range(EXPERTS):
-                first = e * FEAT + j * P
-                nc.tensor.matmul(
-                    out=spread[:, e, :], lhsT=ones_bf[:], rhs=b2_row[:, first : first + P], start=True, stop=True
-                )
-            copy_out(0 if j == 0 else 1, bias_sb[:, j, :, :], spread[:].rearrange("s e d -> s d e"))
-        for piece in range(2):
-            b, m = tiles[len(tiles) - 2 + piece]
+            if i >= 1:
+                quantise_h(*tiles[i - 1], earlier_grouped)
+            earlier_grouped = h_grouped
+        def late_p(piece, i):
             flipped = new_flipped()
             for pair in range(2):
-                transpose_p(b, m, pair, flipped)
-            regroup_p(piece, b, m, flipped)
-        for piece in range(2):
-            quantise_p(*tiles[len(tiles) - 2 + piece])
-        nc.vector.reciprocal(out=inv_sum[:], in_=p_sum[:])
+                transpose_p(*tiles[i], pair, flipped)
+            regroup_p(piece, *tiles[i], flipped)
+            quantise_p(*tiles[i])
+
+        exponential(len(tiles) - 1)
+        quantise_p(*tiles[len(tiles) - 3])
+        quantise_h(*tiles[-1], earlier_grouped)
+        late_p(1, len(tiles) - 2)
 
         blocks = [(b, 2 * half + jj) for half in range(2) for b in range(BATCH) for jj in range(2)]
         for i in range(len(blocks) + COMBINE_LAG):
@@ -320,6 +346,9 @@ def tile_mixtureexpertsmlp_pb_e_kernel(tc, h, w2_words, w2_scales, b2, x, phi, o
                     y_psum = new_y_bank()
                 first_layer_passes(blocks[i][0], blocks[i][1], range(EXPERTS), y_psum)
                 pack_y(blocks[i][0], blocks[i][1], y_psum)
+                if i == 0:
+                    late_p(1, len(tiles) - 1)
+                    nc.vector.reciprocal(out=inv_sum[:], in_=p_sum[:])
             if i >= COMBINE_LAG:
                 b, j = blocks[i - COMBINE_LAG]
                 combine(b, j, i >= len(blocks))

@@ -89,8 +89,7 @@ def tile_mixtureexpertsmlp_pb_e_kernel(tc, h, w2_words, w2_scales, b2, x, phi, o
                     nc.sync.dma_start(out=x_sb[0][:, 2:4, :], in_=x_tiled[0][:, 2:4, :])
                 if (b, e) == (0, 1):
                     nc.sync.dma_start(out=x_sb[1][:], in_=x_tiled[1])
-        for half in range(2):
-            cols = slice(half * (FEAT // 2), (half + 1) * (FEAT // 2))
+        for cols in (slice(0, 2 * P), slice(2 * P, 3 * P), slice(3 * P, 4 * P)):
             for k in range(EXPERTS // 2):
                 groups = slice(2 * k * PASSES, 2 * (k + 1) * PASSES)
                 nc.sync.dma_start(
@@ -337,7 +336,7 @@ def tile_mixtureexpertsmlp_pb_e_kernel(tc, h, w2_words, w2_scales, b2, x, phi, o
         quantise_h(*tiles[-1], earlier_grouped)
         late_p(1, len(tiles) - 2)
 
-        blocks = [(b, 2 * half + jj) for half in range(2) for b in range(BATCH) for jj in range(2)]
+        blocks = [(b, j) for j in range(FEAT_BLOCKS) for b in range(BATCH)]
         for i in range(len(blocks) + COMBINE_LAG):
             if i < len(blocks):
                 if i < COMBINE_LAG:

from contextlib import ExitStack

import concourse.mybir as mybir
from concourse.masks import make_identity

F32 = mybir.dt.float32
BF16 = mybir.dt.bfloat16
I32 = mybir.dt.int32
U32 = mybir.dt.uint32
U8 = mybir.dt.uint8
FP8X4 = mybir.dt.float8_e4m3fn_x4
ALU = mybir.AluOpType
ACT = mybir.ActivationFunctionType
AXIS = mybir.AxisListType

P = 128
PACK = 4
K_PASS = P * PACK

BATCH, EXPERTS, SLOTS, HIDDEN = 2, 4, 128, 2048
TOKENS, FEAT = 512, 512
ALL_SLOTS = EXPERTS * SLOTS
TOKEN_TILES = TOKENS // P
FEAT_BLOCKS = FEAT // P
PASSES = HIDDEN // K_PASS
PASS_WORDS = K_PASS // 2

COMBINE_LAG = 2

FLOPS = 2 * (BATCH * EXPERTS * SLOTS * HIDDEN * FEAT + 2 * BATCH * TOKENS * ALL_SLOTS * FEAT)


def tile_mixtureexpertsmlp_pb_e_kernel(tc, h, w2_words, w2_scales, b2, x, phi, out):
    nc = tc.nc
    with ExitStack() as ctx:
        ctx.enter_context(tc.manual_schedule())
        keep = ctx.enter_context(tc.tile_pool(name="keep", bufs=1))
        stage = ctx.enter_context(tc.tile_pool(name="stage", bufs=3))
        results = ctx.enter_context(tc.tile_pool(name="results", bufs=BATCH * FEAT_BLOCKS))
        psum_small = ctx.enter_context(tc.psum_pool(name="psum_small", bufs=6))
        psum_wide = ctx.enter_context(tc.psum_pool(name="psum_wide", bufs=2))

        def copy_out(piece, out_ap, in_ap):
            if piece % 2 == 0:
                nc.vector.tensor_copy(out=out_ap, in_=in_ap)
            else:
                nc.scalar.copy(out=out_ap, in_=in_ap)

        b2_rows = keep.tile([P, P], BF16, name="b2_rows")
        nc.vector.memset(b2_rows[:].bitcast(I32), 0)
        idle_rhs = keep.tile([P, ALL_SLOTS], BF16, name="idle_rhs")
        nc.vector.memset(idle_rhs[:].bitcast(I32), 0)
        warm = keep.tile([P, 1], F32, name="warm")
        nc.vector.memset(warm[:], 0.0)
        nc.scalar.activation(out=warm[:], in_=warm[:], func=ACT.Exp)
        ident_f32 = keep.tile([P, P], F32, name="ident_f32")
        ident_bf = keep.tile([P, P], BF16, name="ident_bf")
        make_identity(nc, ident_bf[:])
        make_identity(nc, ident_f32[:])
        w_scales = keep.tile([P, EXPERTS, FEAT], U8, name="w_scales", align_bytes=64)
        nc.vector.memset(w_scales[:].rearrange("r e n -> r (e n)").bitcast(I32), 0)

        phi_sb = keep.tile([P, EXPERTS, FEAT], BF16, name="phi_sb")
        x_sb = [keep.tile([P, TOKEN_TILES, FEAT], BF16, name="x_sb%d" % b) for b in range(BATCH)]
        h_sb = [[keep.tile([P, HIDDEN], BF16, name="h_sb%d_%d" % (b, e)) for e in range(EXPERTS)] for b in range(BATCH)]
        w_codes = keep.tile([P, EXPERTS * PASSES, FEAT], U32, name="w_codes", align_bytes=64)
        x_tiled = [x[b].rearrange("(r m) d -> r m d", m=TOKEN_TILES) for b in range(BATCH)]
        nc.sync.dma_start(out=b2_rows[0 : EXPERTS * FEAT_BLOCKS, :], in_=b2.rearrange("e (j d) -> (e j) d", d=P))
        nc.sync.dma_start(out=x_sb[0][:, 0:1, :], in_=x_tiled[0][:, 0:1, :])
        for e in range(EXPERTS):
            k, v = divmod(e, 2)
            nc.sync.dma_start(
                out=phi_sb[v:P:2, 2 * k : 2 * k + 2, :], in_=phi[e].rearrange("(s2 i) d -> i s2 d", s2=2)
            )
        for half in range(2):
            cols = slice(half * (HIDDEN // 2), (half + 1) * (HIDDEN // 2))
            nc.sync.dma_start(out=h_sb[0][0][:, cols], in_=h[0, 0, :, cols])
        nc.sync.dma_start(out=x_sb[0][:, 1:2, :], in_=x_tiled[0][:, 1:2, :])
        for b in range(BATCH):
            for e in range(EXPERTS):
                if (b, e) != (0, 0):
                    nc.sync.dma_start(out=h_sb[b][e][:], in_=h[b, e])
                for quadrant in (2 * b, 2 * b + 1):
                    nc.sync.dma_start(
                        out=w_scales[32 * quadrant : 32 * quadrant + 16, e, :].bitcast(I32),
                        in_=w2_scales[PASSES * e : PASSES * (e + 1), 4 * quadrant : 4 * quadrant + 4, :].bitcast(I32),
                    )
                if (b, e) == (0, 0):
                    nc.sync.dma_start(out=x_sb[0][:, 2:4, :], in_=x_tiled[0][:, 2:4, :])
                if (b, e) == (0, 1):
                    nc.sync.dma_start(out=x_sb[1][:], in_=x_tiled[1])
        for cols in (slice(0, 2 * P), slice(2 * P, 3 * P), slice(3 * P, 4 * P)):
            for k in range(EXPERTS // 2):
                groups = slice(2 * k * PASSES, 2 * (k + 1) * PASSES)
                nc.sync.dma_start(
                    out=w_codes[:, groups, cols].bitcast(I32),
                    in_=w2_words[groups, :, cols, :].rearrange("g r n t -> r g (n t)").bitcast(I32),
                )

        phiT = keep.tile([P, FEAT_BLOCKS, ALL_SLOTS], BF16, name="phiT")
        xT = [keep.tile([P, TOKEN_TILES, 2, P, 2], BF16, name="xT%d" % b) for b in range(BATCH)]
        p_bf = [[keep.tile([P, ALL_SLOTS], BF16, name="p_bf%d_%d" % (b, m)) for m in range(TOKEN_TILES)] for b in range(BATCH)]
        neg_max = keep.tile([P, BATCH * TOKEN_TILES], F32, name="neg_max")
        p_sum = keep.tile([P, BATCH * TOKEN_TILES], F32, name="p_sum")
        inv_sum = keep.tile([P, BATCH * TOKEN_TILES], F32, name="inv_sum")
        p_grouped = [keep.tile([P, TOKEN_TILES, P, PACK], BF16, name="p_grouped%d" % b, align_bytes=64) for b in range(BATCH)]
        p_codes = [keep.tile([P, TOKEN_TILES, P], U32, name="p_codes%d" % b, align_bytes=64) for b in range(BATCH)]
        p_scales = [keep.tile([P, TOKEN_TILES, P], U8, name="p_scales%d" % b, align_bytes=64) for b in range(BATCH)]
        h_codes = [[keep.tile([P, PASSES, P], U32, name="h_codes%d_%d" % (b, e), align_bytes=64) for e in range(EXPERTS)] for b in range(BATCH)]
        h_scales = [[keep.tile([P, PASSES, P], U8, name="h_scales%d_%d" % (b, e), align_bytes=64) for e in range(EXPERTS)] for b in range(BATCH)]
        bias_sb = keep.tile([P, FEAT_BLOCKS, P, EXPERTS], F32, name="bias_sb")
        y_codes = [[keep.tile([P, P], U32, name="y_codes%d_%d" % (b, j), align_bytes=64) for j in range(FEAT_BLOCKS)] for b in range(BATCH)]
        y_scales = [[keep.tile([P, P], U8, name="y_scales%d_%d" % (b, j), align_bytes=64) for j in range(FEAT_BLOCKS)] for b in range(BATCH)]

        def new_flipped():
            return psum_small.tile([P, 2, P], F32, tag="small", name="flipped")

        def transpose_phi(q, u, flipped):
            nc.tensor.transpose(flipped[:, u, :], phi_sb[:, q, :].bitcast(F32)[:, u * P : (u + 1) * P], ident_f32[:])

        def transpose_x(b, m, u, flipped):
            nc.tensor.transpose(flipped[:, u, :], x_sb[b][:, m, :].bitcast(F32)[:, u * P : (u + 1) * P], ident_f32[:])

        def keep_x(b, m, flipped):
            nc.vector.tensor_copy(
                out=xT[b][:, m, :, :, :].rearrange("d u r v -> d (u r v)").bitcast(F32), in_=flipped[:].rearrange("d u r -> d (u r)")
            )

        def transpose_p(b, m, pair, flipped):
            nc.tensor.transpose(flipped[:, pair, :], p_bf[b][m][:].bitcast(F32)[:, pair * P : (pair + 1) * P], ident_f32[:])

        def regroup_p(piece, b, m, flipped):
            copy_out(piece, p_grouped[b][:, m, :, :].bitcast(F32), flipped[:].rearrange("s pair r -> s r pair"))

        def quantise_p(b, m):
            nc.vector.quantize_mx(
                out=p_codes[b][:, m, :].bitcast(FP8X4),
                scales=p_scales[b][:, m, :],
                in_=p_grouped[b][:, m, :, :].rearrange("s r e -> s (r e)"),
            )

        def new_flipped_words():
            return psum_small.tile([P, 2, 2, P], F32, tag="small", name="flipped_words")

        def transpose_h(b, e, g, u, flipped):
            nc.tensor.transpose(
                flipped[:, g % 2, u, :],
                h_sb[b][e][:].bitcast(F32)[:, PASS_WORDS * g + u : PASS_WORDS * (g + 1) : 2],
                ident_f32[:],
            )

        def regroup_h(half, grouped, flipped):
            nc.scalar.copy(
                out=grouped[:, 2 * half : 2 * half + 2, :, :].bitcast(F32),
                in_=flipped[:].rearrange("r g u s -> r g s u"),
            )

        def quantise_h(b, e, grouped):
            nc.vector.quantize_mx(
                out=h_codes[b][e][:].rearrange("r g s -> r (g s)").bitcast(FP8X4),
                scales=h_scales[b][e][:].rearrange("r g s -> r (g s)"),
                in_=grouped[:].rearrange("r g s t -> r (g s t)"),
            )

        def new_y_bank():
            return psum_small.tile([P, EXPERTS, P], F32, tag="small", name="y_psum")

        def first_layer_passes(b, j, experts, y_psum):
            cols = slice(j * P, (j + 1) * P)
            for e in experts:
                for g in range(PASSES):
                    nc.tensor.matmul_mx(
                        out=y_psum[:, e, :],
                        lhsT=h_codes[b][e][:, g, :].bitcast(FP8X4),
                        lhsT_scale=h_scales[b][e][:, g, :],
                        rhs=w_codes[:, PASSES * e + g, cols].bitcast(FP8X4),
                        rhs_scale=w_scales[4 * g : P, e, cols],
                        start=(g == 0),
                        stop=(g == PASSES - 1),
                    )

        def pack_y(b, j, y_psum):
            y_grouped = stage.tile([P, P, PACK], BF16, name="y_grouped", align_bytes=64)
            nc.vector.tensor_tensor(
                out=y_grouped[:], in0=y_psum[:].rearrange("s e d -> s d e"), in1=bias_sb[:, j, :, :], op=ALU.add
            )
            nc.vector.quantize_mx(
                out=y_codes[b][j][:].bitcast(FP8X4),
                scales=y_scales[b][j][:],
                in_=y_grouped[:].rearrange("s d e -> s (d e)"),
            )

        def combine(b, j, vector_helps):
            result = results.tile([P, TOKEN_TILES, P], F32, name="result")
            for half in range(2):
                if half == 0:
                    combined = psum_wide.tile([P, 2, P], F32, tag="wide", name="combined")
                else:
                    combined = psum_small.tile([P, 2, P], F32, tag="small", name="combined")
                for mm in range(2):
                    m = 2 * half + mm
                    nc.tensor.matmul_mx(
                        out=combined[:, mm, :],
                        lhsT=p_codes[b][:, m, :].bitcast(FP8X4),
                        lhsT_scale=p_scales[b][:, m, :],
                        rhs=y_codes[b][j][:].bitcast(FP8X4),
                        rhs_scale=y_scales[b][j][:],
                        start=True,
                        stop=True,
                    )
                for mm in range(2):
                    m = 2 * half + mm
                    col = b * TOKEN_TILES + m
                    if half == 0 or not vector_helps:
                        nc.scalar.activation(
                            out=result[:, m, :], in_=combined[:, mm, :], func=ACT.Copy, scale=inv_sum[:, col : col + 1]
                        )
                    else:
                        nc.vector.tensor_scalar_mul(
                            out=result[:, m, :], in0=combined[:, mm, :], scalar1=inv_sum[:, col : col + 1]
                        )
                nc.sync.dma_start(
                    out=out[b].rearrange("(r m) d -> r m d", m=TOKEN_TILES)[:, 2 * half : 2 * half + 2, j * P : (j + 1) * P],
                    in_=result[:, 2 * half : 2 * half + 2, :],
                )

        def keep_busy(count):
            unread = psum_wide.tile([P, ALL_SLOTS], F32, tag="wide", name="unread")
            for k in range(count):
                nc.tensor.matmul(out=unread[:], lhsT=idle_rhs[:, 0:P], rhs=idle_rhs[:], start=True, stop=True)

        def spread_bias(j, spread):
            for e in range(EXPERTS):
                row = e * FEAT_BLOCKS + j
                nc.tensor.matmul(
                    out=spread[:, e, :], lhsT=ident_bf[:, row : row + 1].to_broadcast([P, P]), rhs=b2_rows[:], start=True, stop=True
                )
            return spread

        def keep_bias(piece, j, spread):
            copy_out(piece, bias_sb[:, j, :, :], spread[:].rearrange("s e d -> s d e"))

        def wide_bank():
            return psum_wide.tile([P, EXPERTS, P], F32, tag="wide", name="bias_wide")

        def small_bank():
            return psum_small.tile([P, EXPERTS, P], F32, tag="small", name="bias_small")

        def phi_tile(q):
            for u in range(2):
                flipped = new_flipped()
                transpose_phi(q, u, flipped)
                copy_out(
                    u,
                    phiT[:, 2 * u : 2 * u + 2, q * P : (q + 1) * P],
                    flipped[:, u, :].bitcast(BF16).rearrange("d (s v) -> d v s", v=2),
                )

        keep_busy(4)
        spreads = [spread_bias(j, wide_bank()) for j in range(2)]
        flipped = new_flipped()
        for u in range(2):
            transpose_x(0, 0, u, flipped)
        keep_x(0, 0, flipped)
        keep_bias(1, 0, spreads[0])
        phi_tile(0)
        phi_tile(1)
        spreads.append(spread_bias(2, small_bank()))
        phi_tile(2)
        phi_tile(3)
        spreads.append(spread_bias(3, small_bank()))
        keep_bias(0, 1, spreads[1])
        keep_bias(1, 2, spreads[2])
        keep_bias(0, 3, spreads[3])

        tiles = [(b, m) for b in range(BATCH) for m in range(TOKEN_TILES)]

        def exponential(i):
            b, m = tiles[i]
            nc.scalar.activation(
                out=p_bf[b][m][:], in_=all_logits[i][:], func=ACT.Exp,
                bias=neg_max[:, i : i + 1], scale=1.0, accum_out=p_sum[:, i : i + 1],
            )

        all_logits = []
        for i in range(len(tiles)):
            b, m = tiles[i]
            following = tiles[i + 1] if i + 1 < len(tiles) else None
            earlier = tiles[i - 2] if i >= 2 else None
            logits = psum_wide.tile([P, ALL_SLOTS], F32, tag="wide", name="logits")
            all_logits.append(logits)
            h_grouped = stage.tile([P, PASSES, P, PACK], BF16, name="h_grouped", align_bytes=64)
            x_round = 1 if i == 0 else 0
            for c in range(FEAT_BLOCKS):
                nc.tensor.matmul(
                    out=logits[:], lhsT=xT[b][:, m, c // 2, :, c % 2], rhs=phiT[:, c, :],
                    start=(c == 0), stop=(c == FEAT_BLOCKS - 1),
                )
                if c == x_round and following is not None:
                    flipped_x = new_flipped()
                if c == 2 and earlier is not None:
                    flipped_p = new_flipped()
                if c in (x_round, x_round + 1) and following is not None:
                    transpose_x(following[0], following[1], c - x_round, flipped_x)
                if c >= 2 and earlier is not None:
                    transpose_p(earlier[0], earlier[1], c - 2, flipped_p)
                if c % 2 == 0:
                    flipped_words = new_flipped_words()
                for u in range(2):
                    transpose_h(b, m, c, u, flipped_words)
                if c == 0 and i >= 1:
                    exponential(i - 1)
                if c == x_round + 1 and following is not None:
                    keep_x(following[0], following[1], flipped_x)
                if c == 1 and i >= 3:
                    quantise_p(*tiles[i - 3])
                if c % 2 == 1:
                    regroup_h(c // 2, h_grouped, flipped_words)
            nc.vector.tensor_reduce(
                out=neg_max[:, i : i + 1], in_=logits[:], axis=AXIS.X, op=ALU.max, negate=True
            )
            if earlier is not None:
                regroup_p(0, earlier[0], earlier[1], flipped_p)
            if i >= 1:
                quantise_h(*tiles[i - 1], earlier_grouped)
            earlier_grouped = h_grouped
        def late_p(piece, i):
            flipped = new_flipped()
            for pair in range(2):
                transpose_p(*tiles[i], pair, flipped)
            regroup_p(piece, *tiles[i], flipped)
            quantise_p(*tiles[i])

        exponential(len(tiles) - 1)
        quantise_p(*tiles[len(tiles) - 3])
        quantise_h(*tiles[-1], earlier_grouped)
        late_p(1, len(tiles) - 2)

        blocks = [(b, j) for j in range(FEAT_BLOCKS) for b in range(BATCH)]
        for i in range(len(blocks) + COMBINE_LAG):
            if i < len(blocks):
                if i < COMBINE_LAG:
                    y_psum = psum_wide.tile([P, EXPERTS, P], F32, tag="wide", name="y_psum_first")
                else:
                    y_psum = new_y_bank()
                first_layer_passes(blocks[i][0], blocks[i][1], range(EXPERTS), y_psum)
                pack_y(blocks[i][0], blocks[i][1], y_psum)
                if i == 0:
                    late_p(1, len(tiles) - 1)
                    nc.vector.reciprocal(out=inv_sum[:], in_=p_sum[:])
            if i >= COMBINE_LAG:
                b, j = blocks[i - COMBINE_LAG]
                combine(b, j, i >= len(blocks))
